import numpy as np
import ml_dtypes


def mxq(x, axis, fmt="e4m3"):
    dtype, down = {"e4m3": (ml_dtypes.float8_e4m3fn, 7), "e5m2": (ml_dtypes.float8_e5m2, 14)}[fmt]
    v = np.moveaxis(np.asarray(x, np.float32).astype(ml_dtypes.bfloat16).astype(np.float64), axis, -1)
    blocks = v.reshape(v.shape[:-1] + (-1, 32))
    amax = np.abs(blocks).max(-1, keepdims=True)
    byte = np.maximum(np.where(amax > 0, np.frexp(amax)[1] - 1 + 127, 0) - down, 1)
    scale = np.exp2(byte - 127.0)
    codes = (blocks / scale).astype(np.float32).astype(dtype).astype(np.float64)
    return np.moveaxis((codes * scale).reshape(v.shape), -1, axis)


WIDE = False


def mx_kscale(k):
    if not WIDE:
        return np.ones(k)
    levels = np.array([10, -10, 5, -5, 0])
    if k % 512:
        return np.exp2(np.random.permutation(np.resize(levels, k // 32))).repeat(32)
    a = np.empty((k // 512, 16))
    for p in range(k // 512):
        a[p, :8] = np.random.permutation(np.resize(levels, 8))
        for g in range(8):
            far = levels[np.abs(levels - a[p, g]) >= 10]
            a[p, g + 8] = far[np.random.randint(len(far))]
    return np.exp2(a.ravel()).repeat(32)


BF16 = ml_dtypes.bfloat16


def bf(x):
    return np.asarray(x, np.float32).astype(BF16)


def f64(x):
    return np.asarray(x).astype(np.float64)


B, S, D = 2, 1024, 1024
EPS = 1e-8


def layer_norm(v, w, b):
    mu = v.mean(-1, keepdims=True)
    var = ((v - mu) ** 2).mean(-1, keepdims=True)
    return (v - mu) / np.sqrt(var + EPS) * w + b


def setup_inputs():
    s = mx_kscale(D)
    xr = np.random.standard_normal((B, S, D)) + np.random.uniform(-1.2, 1.2, (B, S, 1))
    xi = np.random.standard_normal((B, S, D)) + np.random.uniform(-1.2, 1.2, (B, S, 1))
    return {"x_real": bf(xr * s), "x_imag": bf(xi * s),
            "phase_matrix": bf(np.random.standard_normal((D, D)) / np.sqrt(D) / s[:, None]),
            "coherence_factor": bf(np.random.uniform(0.35, 0.5, 1)),
            "ln_weight": bf(1.0 + 0.1 * np.random.standard_normal(D)),
            "ln_bias": bf(0.3 * np.random.standard_normal(D))}


def reference(x_real, x_imag, phase_matrix, coherence_factor, ln_weight, ln_bias):
    xr, xi = f64(x_real), f64(x_imag)
    a, b = xr + EPS, xi + EPS
    r = np.sqrt(a * a + b * b)
    sc = (a / r).sum(-1, keepdims=True)
    ss = (b / r).sum(-1, keepdims=True)
    coherence = (sc * sc + ss * ss) / (D * D)
    p = mxq(xr, 2, "e4m3") @ mxq(f64(phase_matrix), 0, "e4m3")
    p = p * f64(coherence_factor) * (1.0 - coherence)
    c, sn = np.cos(p), np.sin(p)
    new_real = xr * c - xi * sn
    new_imag = xr * sn + xi * c
    norm = np.sqrt(new_real ** 2 + new_imag ** 2 + EPS)
    new_real = new_real / norm
    new_imag = new_imag / norm
    w, bb = f64(ln_weight), f64(ln_bias)
    return (layer_norm(new_real, w, bb), layer_norm(new_imag, w, bb))

@@ -1,0 +1,376 @@
+import math
+from contextlib import ExitStack
+
+import concourse.mybir as mybir
+from concourse.masks import make_identity
+
+F32 = mybir.dt.float32
+BF16 = mybir.dt.bfloat16
+I32 = mybir.dt.int32
+U32 = mybir.dt.uint32
+U8 = mybir.dt.uint8
+FP8X4 = mybir.dt.float8_e4m3fn_x4
+ACT = mybir.ActivationFunctionType
+ALU = mybir.AluOpType
+
+P = 128
+D = 1024
+ROWS = 2048
+NT = ROWS // P
+BANK = 512
+PASSES = D // 512
+BLOCKS = D // P
+EPS = 1e-8
+POOL_COLS = 768
+FLOPS = 2 * ROWS * D * D
+
+
+def tile_quantumcoherencelayer_kernel(
+    tc, x_real, x_imag, phase_matrix, coherence_factor, ln_weight, ln_bias, out_0, out_1
+):
+    nc = tc.nc
+    xr_d = x_real.flatten_outer_dims().rearrange("(t p) d -> t p d", p=P)
+    xi_d = x_imag.flatten_outer_dims().rearrange("(t p) d -> t p d", p=P)
+    o0_d = out_0.flatten_outer_dims().rearrange("(t p) d -> t p d", p=P)
+    o1_d = out_1.flatten_outer_dims().rearrange("(t p) d -> t p d", p=P)
+
+    with ExitStack() as ctx:
+        keep = ctx.enter_context(tc.tile_pool(name="keep", bufs=1))
+        cpsum = ctx.enter_context(tc.psum_pool(name="cpsum", bufs=1))
+
+        ident = keep.tile([P, P], F32)
+        make_identity(nc, ident[:])
+        eps_t = keep.tile([P, 1], F32)
+        nc.vector.memset(eps_t[:], EPS)
+        neghalf = keep.tile([P, 2], F32)
+        nc.vector.memset(neghalf[:], -0.5)
+
+        cf_bf = keep.tile([P, 1], BF16)
+        with nc.allow_non_contiguous_dma(reason="one bfloat16 scalar to every partition"):
+            nc.scalar.dma_start(out=cf_bf[:], in_=coherence_factor.partition_broadcast(P))
+        cf = keep.tile([P, 1], F32)
+        nc.vector.tensor_copy(out=cf[:], in_=cf_bf[:])
+
+        p_codes = keep.tile([P, PASSES, D], U32, align_bytes=64)
+        p_scales = keep.tile([P, PASSES, D], U8, align_bytes=64)
+        x_codes = keep.tile([P, NT, PASSES * P], U32, align_bytes=64)
+        x_scales = keep.tile([P, NT, PASSES * P], U8, align_bytes=64)
+        sum_cos = keep.tile([P, NT], F32)
+        sum_sin = keep.tile([P, NT], F32)
+        gain = keep.tile([P, NT], F32)
+        wb_cols = keep.tile([P, 2 * BLOCKS], F32)
+        unit_re = [keep.tile([P, D], F32, name="cr%d" % i) for i in range(NT)]
+        unit_im_neg = [keep.tile([P, D], F32, name="nci%d" % i) for i in range(NT)]
+
+        w_ps = cpsum.tile([P, D], BF16)
+        b_ps = cpsum.tile([P, D], BF16)
+
+        with tc.tile_pool(name="stage", bufs=1) as stage, tc.tile_pool(name="xin", bufs=3) as xin, tc.tile_pool(
+            name="worka", bufs=2
+        ) as worka, tc.psum_pool(name="tpsum", bufs=2) as tpsum:
+            rows = stage.tile([P, 2 * D], BF16)
+            nc.vector.memset(rows[:], 0.0)
+            nc.scalar.dma_start(out=rows[0:1, 0:D], in_=ln_weight.rearrange("(o d) -> o d", o=1))
+            nc.scalar.dma_start(out=rows[0:1, D : 2 * D], in_=ln_bias.rearrange("(o d) -> o d", o=1))
+            ones = stage.tile([P, P], BF16)
+            nc.vector.memset(ones[:], 1.0)
+            for h in range(2):
+                nc.tensor.matmul(
+                    out=w_ps[:, h * BANK : (h + 1) * BANK],
+                    lhsT=ones[:],
+                    rhs=rows[:, h * BANK : (h + 1) * BANK],
+                    start=True,
+                    stop=True,
+                )
+            for h in range(2):
+                nc.tensor.matmul(
+                    out=b_ps[:, h * BANK : (h + 1) * BANK],
+                    lhsT=ones[:],
+                    rhs=rows[:, D + h * BANK : D + (h + 1) * BANK],
+                    start=True,
+                    stop=True,
+                )
+
+            wb = stage.tile([P, P], BF16)
+            nc.vector.memset(wb[:], 0.0)
+            nc.scalar.dma_start(out=wb[0:BLOCKS, :], in_=ln_weight.rearrange("(j p) -> j p", p=P))
+            nc.scalar.dma_start(out=wb[BLOCKS : 2 * BLOCKS, :], in_=ln_bias.rearrange("(j p) -> j p", p=P))
+            wb32 = stage.tile([P, P], F32)
+            nc.vector.tensor_copy(out=wb32[:], in_=wb[:])
+            wbt_ps = tpsum.tile([P, BANK], F32, tag="xt")
+            nc.tensor.transpose(out=wbt_ps[:, 0:P], in_=wb32[:], identity=ident[:])
+            nc.vector.tensor_copy(out=wb_cols[:], in_=wbt_ps[:, 0 : 2 * BLOCKS])
+
+            for i in range(NT):
+                xr = xin.tile([P, D], BF16, tag="xr")
+                nc.sync.dma_start(out=xr[:], in_=xr_d[i])
+                xi = xin.tile([P, D], BF16, tag="xi")
+                nc.sync.dma_start(out=xi[:], in_=xi_d[i])
+
+                if i == 1:
+                    for g in range(PASSES):
+                        raw = stage.tile([P, 4, D], BF16, tag="raw")
+                        nc.sync.dma_start(
+                            out=raw[:],
+                            in_=phase_matrix[512 * g : 512 * (g + 1), :].rearrange("(q t) c -> q t c", t=4),
+                        )
+                        pg = stage.tile([P, D, 4], BF16, tag="pg", align_bytes=64)
+                        nc.vector.tensor_copy(
+                            out=pg[:].rearrange("p (c i) t -> p c t i", i=4),
+                            in_=raw[:].rearrange("p t (c i) -> p c t i", i=4),
+                        )
+                        nc.vector.quantize_mx(
+                            out=p_codes[:, g, :].bitcast(FP8X4),
+                            scales=p_scales[:, g, :],
+                            in_=pg[:].rearrange("p c t -> p (c t)"),
+                        )
+
+                xt = tpsum.tile([P, BANK], F32, tag="xt")
+                xw = xr[:].bitcast(F32)
+                for j in range(4):
+                    g, u = divmod(j, 2)
+                    nc.tensor.transpose(
+                        out=xt[:, j * P : (j + 1) * P], in_=xw[:, 256 * g + u : 256 * (g + 1) : 2], identity=ident[:]
+                    )
+                grouped = worka.tile([P, PASSES, P, 4], BF16, tag="grouped", align_bytes=64)
+                nc.scalar.copy(
+                    out=grouped[:].bitcast(F32),
+                    in_=xt[:].rearrange("p (g u r) -> p g r u", g=PASSES, u=2),
+                )
+
+                inv_r = worka.tile([P, D], F32, tag="sa")
+                scr_a = worka.tile([P, D], F32, tag="sb")
+                inv_n = worka.tile([P, D], F32, tag="sr")
+                scr_b = worka.tile([P, D], F32, tag="si")
+                nc.scalar.activation(out=inv_r[:], in_=xr[:], func=ACT.Square, bias=eps_t[:, 0:1], scale=1.0)
+                nc.scalar.activation(out=scr_a[:], in_=xi[:], func=ACT.Square, bias=eps_t[:, 0:1], scale=1.0)
+                nc.scalar.activation(out=inv_n[:], in_=xr[:], func=ACT.Square)
+                nc.scalar.activation(out=scr_b[:], in_=xi[:], func=ACT.Square)
+                nc.vector.tensor_tensor(out=inv_r[:], in0=inv_r[:], in1=scr_a[:], op=ALU.add)
+                nc.vector.tensor_tensor(out=inv_n[:], in0=inv_n[:], in1=scr_b[:], op=ALU.add)
+                nc.vector.quantize_mx(
+                    out=x_codes[:, i, :].bitcast(FP8X4),
+                    scales=x_scales[:, i, :],
+                    in_=grouped[:].rearrange("p g r t -> p (g r t)"),
+                )
+                nc.scalar.activation(out=inv_r[:], in_=inv_r[:], func=ACT.Abs_reciprocal_sqrt)
+                nc.scalar.activation(
+                    out=inv_n[:], in_=inv_n[:], func=ACT.Abs_reciprocal_sqrt, bias=eps_t[:, 0:1], scale=1.0
+                )
+                nc.vector.scalar_tensor_tensor(
+                    out=scr_a[:], in0=xr[:], scalar=EPS, in1=inv_r[:], op0=ALU.add, op1=ALU.mult,
+                    accum_out=sum_cos[:, i : i + 1],
+                )
+                nc.vector.scalar_tensor_tensor(
+                    out=scr_b[:], in0=xi[:], scalar=EPS, in1=inv_r[:], op0=ALU.add, op1=ALU.mult,
+                    accum_out=sum_sin[:, i : i + 1],
+                )
+                nc.vector.tensor_tensor(out=unit_re[i][:], in0=xr[:], in1=inv_n[:], op=ALU.mult)
+                nc.vector.scalar_tensor_tensor(
+                    out=unit_im_neg[i][:], in0=xi[:], scalar=-1.0, in1=inv_n[:], op0=ALU.mult, op1=ALU.mult
+                )
+
+            nc.vector.tensor_tensor(out=sum_cos[:], in0=sum_cos[:], in1=sum_cos[:], op=ALU.mult)
+            nc.vector.tensor_tensor(out=sum_sin[:], in0=sum_sin[:], in1=sum_sin[:], op=ALU.mult)
+            nc.vector.tensor_tensor(out=sum_cos[:], in0=sum_cos[:], in1=sum_sin[:], op=ALU.add)
+            nc.vector.tensor_scalar(
+                out=sum_cos[:], in0=sum_cos[:], scalar1=-1.0 / (D * D), scalar2=1.0, op0=ALU.mult, op1=ALU.add
+            )
+            nc.vector.tensor_scalar(
+                out=gain[:], in0=sum_cos[:], scalar1=cf[:, 0:1], scalar2=1.0 / (2.0 * math.pi), op0=ALU.mult,
+                op1=ALU.mult,
+            )
+
+        with tc.tile_pool(name="workb", bufs=2) as workb, tc.tile_pool(name="stat", bufs=4) as stat, tc.psum_pool(
+            name="ppsum", bufs=2
+        ) as ppsum, tc.manual_schedule():
+            p0 = {}
+            sine = {}
+            vers = {}
+            out_re = {}
+            cos_im = {}
+            rot_im = {}
+            rot_re = {}
+            sums = {}
+            neg_mean = {}
+            sq_dev = {}
+            var_eps = {}
+            inv_std = {}
+            turned_im = {}
+
+            def valid(i):
+                return 0 <= i < NT
+
+            def turned(i):
+                return 0 <= i < NT - 1
+
+            def product(i):
+                p0[i] = [ppsum.tile([P, BANK], F32, name="p0_%d" % n, tag="p0_%d" % n) for n in range(2)]
+                for n in range(2):
+                    for g in range(PASSES):
+                        nc.tensor.matmul_mx(
+                            out=p0[i][n][:],
+                            lhsT=x_codes[:, i, g * P : (g + 1) * P].bitcast(FP8X4),
+                            lhsT_scale=x_scales[:, i, g * P : (g + 1) * P],
+                            rhs=p_codes[:, g, n * BANK : (n + 1) * BANK].bitcast(FP8X4),
+                            rhs_scale=p_scales[:, g, n * BANK : (n + 1) * BANK],
+                            start=(g == 0),
+                            stop=(g == PASSES - 1),
+                        )
+
+            def reduce_range(i):
+                g_i = gain[:, i : i + 1]
+                nearest = workb.tile([P, D], I32, name="ki", tag="ki", bufs=1)
+                sine[i] = workb.tile([P, D], F32, name="vs", tag="vs")
+                for n in range(2):
+                    cols = slice(n * BANK, (n + 1) * BANK)
+                    nc.vector.tensor_scalar(
+                        out=nearest[:, cols], in0=p0[i][n][:], scalar1=g_i, scalar2=None, op0=ALU.mult
+                    )
+                for n in range(2):
+                    cols = slice(n * BANK, (n + 1) * BANK)
+                    nc.vector.scalar_tensor_tensor(
+                        out=sine[i][:, cols], in0=p0[i][n][:], scalar=g_i, in1=nearest[:, cols], op0=ALU.mult,
+                        op1=ALU.subtract,
+                    )
+
+            def two_sines(i):
+                vers[i] = workb.tile([P, D], F32, name="hh", tag="hh")
+                nc.scalar.activation(out=vers[i][:], in_=sine[i][:], func=ACT.Sin, scale=math.pi)
+                nc.scalar.activation(out=sine[i][:], in_=sine[i][:], func=ACT.Sin, scale=2.0 * math.pi)
+
+            def versine(i):
+                nc.scalar.activation(out=vers[i][:], in_=vers[i][:], func=ACT.Square, scale=math.sqrt(2.0))
+
+            def cosine_products_and_real_part(i):
+                out_re[i] = workb.tile([P, D], F32, name="fa", tag="fa", bufs=3)
+                cos_im[i] = workb.tile([P, D], F32, name="fb", tag="o%d" % (i % 4), bufs=1)
+                nc.vector.scalar_tensor_tensor(
+                    out=out_re[i][:], in0=vers[i][:], scalar=1.0, in1=unit_re[i][:], op0=ALU.subtract, op1=ALU.mult
+                )
+                nc.vector.scalar_tensor_tensor(
+                    out=cos_im[i][:], in0=vers[i][:], scalar=1.0, in1=unit_im_neg[i][:], op0=ALU.subtract, op1=ALU.mult
+                )
+                sums[i] = stat.tile([P, 2], F32, name="sums", tag="sums")
+                nc.vector.scalar_tensor_tensor(
+                    out=rot_re[i][:], in0=rot_re[i][:], scalar=1.0, in1=out_re[i][:], op0=ALU.mult, op1=ALU.subtract,
+                    accum_out=sums[i][:, 0:1],
+                )
+
+            def sine_product_re_on_vector(i):
+                rot_re[i] = workb.tile([P, D], F32, name="sb2", tag="sb2", bufs=3)
+                nc.vector.tensor_tensor(
+                    out=rot_re[i][:, POOL_COLS:D], in0=sine[i][:, POOL_COLS:D], in1=unit_im_neg[i][:, POOL_COLS:D],
+                    op=ALU.mult,
+                )
+
+            def normalise_im(i):
+                nc.vector.tensor_scalar(
+                    out=rot_im[i][:], in0=rot_im[i][:], scalar1=neg_mean[i][:, 1:2], scalar2=inv_std[i][:, 1:2],
+                    op0=ALU.add, op1=ALU.mult,
+                )
+
+            def imaginary_part_and_means(i):
+                nc.vector.scalar_tensor_tensor(
+                    out=rot_im[i][:], in0=rot_im[i][:], scalar=1.0, in1=cos_im[i][:], op0=ALU.mult, op1=ALU.add,
+                    accum_out=sums[i][:, 1:2],
+                )
+                neg_mean[i] = stat.tile([P, 2], F32, name="nmu", tag="nmu")
+                nc.vector.tensor_scalar(
+                    out=neg_mean[i][:], in0=sums[i][:], scalar1=-1.0 / D, scalar2=None, op0=ALU.mult
+                )
+
+            def variances(i):
+                sq_dev[i] = stat.tile([P, 2], F32, name="sq", tag="sq")
+                nc.scalar.activation(
+                    out=vers[i][:], in_=rot_re[i][:], func=ACT.Square, bias=neg_mean[i][:, 0:1], scale=1.0,
+                    accum_out=sq_dev[i][:, 0:1],
+                )
+                nc.scalar.activation(
+                    out=vers[i][:], in_=rot_im[i][:], func=ACT.Square, bias=neg_mean[i][:, 1:2], scale=1.0,
+                    accum_out=sq_dev[i][:, 1:2],
+                )
+                var_eps[i] = stat.tile([P, 2], F32, name="var", tag="var")
+                nc.scalar.activation(
+                    out=var_eps[i][:], in_=sq_dev[i][:], func=ACT.Identity, bias=eps_t[:, 0:1], scale=1.0 / D
+                )
+
+            def sine_products_on_gpsimd(i):
+                rot_im[i] = workb.tile([P, D], F32, name="sa2", tag="o%d" % ((i - 1) % 4), bufs=1)
+                nc.gpsimd.tensor_tensor(out=rot_im[i][:], in0=sine[i][:], in1=unit_re[i][:], op=ALU.mult)
+                nc.gpsimd.tensor_tensor(
+                    out=rot_re[i][:, 0:POOL_COLS], in0=sine[i][:, 0:POOL_COLS], in1=unit_im_neg[i][:, 0:POOL_COLS],
+                    op=ALU.mult,
+                )
+
+            def inverse_deviations(i):
+                inv_std[i] = stat.tile([P, 2], F32, name="rstd", tag="rstd")
+                nc.gpsimd.tensor_tensor(out=inv_std[i][:], in0=var_eps[i][:], in1=neghalf[:], op=ALU.pow)
+
+            def scale_shift(dst, src, i, c):
+                nc.vector.scalar_tensor_tensor(
+                    out=dst[:], in0=src[:], scalar=neg_mean[i][:, c : c + 1], in1=w_ps[:], op0=ALU.add, op1=ALU.mult
+                )
+                nc.vector.scalar_tensor_tensor(
+                    out=dst[:], in0=dst[:], scalar=inv_std[i][:, c : c + 1], in1=b_ps[:], op0=ALU.mult, op1=ALU.add
+                )
+
+            def there(i, half):
+                t1 = ppsum.tile([P, BANK], F32, name="t1", tag="t1", bufs=1)
+                for jj in range(4):
+                    j = 4 * half + jj
+                    nc.tensor.transpose(
+                        out=t1[:, jj * P : (jj + 1) * P], in_=rot_im[i][:, j * P : (j + 1) * P], identity=ident[:]
+                    )
+                for jj in range(4):
+                    j = 4 * half + jj
+                    nc.scalar.activation(
+                        out=turned_im[i][:, j, :], in_=t1[:, jj * P : (jj + 1) * P], func=ACT.Identity,
+                        bias=wb_cols[:, BLOCKS + j : BLOCKS + j + 1], scale=wb_cols[:, j : j + 1],
+                    )
+
+            def back(i, half):
+                t2 = ppsum.tile([P, BANK], F32, name="t2", tag="t2", bufs=1)
+                for jj in range(4):
+                    j = 4 * half + jj
+                    nc.tensor.transpose(out=t2[:, jj * P : (jj + 1) * P], in_=turned_im[i][:, j, :], identity=ident[:])
+                nc.scalar.copy(out=rot_im[i][:, half * BANK : (half + 1) * BANK], in_=t2[:])
+
+            for k in range(-3, NT + 1):
+                if valid(k + 1):
+                    two_sines(k + 1)
+                if turned(k - 2):
+                    back(k - 2, 1)
+                    nc.sync.dma_start(out=o1_d[k - 2], in_=rot_im[k - 2][:])
+                if valid(k):
+                    cosine_products_and_real_part(k)
+                if valid(k + 1):
+                    sine_product_re_on_vector(k + 1)
+                if turned(k - 1):
+                    normalise_im(k - 1)
+                if valid(k):
+                    imaginary_part_and_means(k)
+                if valid(k + 1):
+                    versine(k + 1)
+                if turned(k - 1):
+                    turned_im[k - 1] = workb.tile([P, BLOCKS, P], F32, name="ot", tag="ot", bufs=1)
+                    there(k - 1, 0)
+                if valid(k + 3):
+                    product(k + 3)
+                if valid(k):
+                    variances(k)
+                if turned(k - 1):
+                    back(k - 1, 0)
+                    there(k - 1, 1)
+                if valid(k - 1):
+                    scale_shift(out_re[k - 1], rot_re[k - 1], k - 1, 0)
+                    nc.sync.dma_start(out=o0_d[k - 1], in_=out_re[k - 1][:])
+                if k - 1 == NT - 1:
+                    scale_shift(rot_im[k - 1], rot_im[k - 1], k - 1, 1)
+                    nc.sync.dma_start(out=o1_d[k - 1], in_=rot_im[k - 1][:])
+                if valid(k + 1):
+                    sine_products_on_gpsimd(k + 1)
+                if valid(k):
+                    inverse_deviations(k)
+                if valid(k + 2):
+                    reduce_range(k + 2)

@@ -21,7 +21,7 @@ BANK = 512
 PASSES = D // 512
 BLOCKS = D // P
 EPS = 1e-8
-POOL_COLS = 768
+POOL_COLS = 896
 FLOPS = 2 * ROWS * D * D
 
 

@@ -22,6 +22,7 @@ PASSES = D // 512
 BLOCKS = D // P
 EPS = 1e-8
 POOL_COLS = 896
+AHEAD = 2
 FLOPS = 2 * ROWS * D * D
 
 
@@ -44,12 +45,13 @@ def tile_quantumcoherencelayer_kernel(
         nc.vector.memset(eps_t[:], EPS)
         neghalf = keep.tile([P, 2], F32)
         nc.vector.memset(neghalf[:], -0.5)
+        warm = keep.tile([P, 1], F32)
+        nc.scalar.activation(out=warm[:], in_=eps_t[:], func=ACT.Abs_reciprocal_sqrt)
 
         cf_bf = keep.tile([P, 1], BF16)
-        with nc.allow_non_contiguous_dma(reason="one bfloat16 scalar to every partition"):
-            nc.scalar.dma_start(out=cf_bf[:], in_=coherence_factor.partition_broadcast(P))
         cf = keep.tile([P, 1], F32)
-        nc.vector.tensor_copy(out=cf[:], in_=cf_bf[:])
+        cf_turns = keep.tile([P, 1], F32)
+        cf_slope = keep.tile([P, 1], F32)
 
         p_codes = keep.tile([P, PASSES, D], U32, align_bytes=64)
         p_scales = keep.tile([P, PASSES, D], U8, align_bytes=64)
@@ -60,46 +62,104 @@ def tile_quantumcoherencelayer_kernel(
         gain = keep.tile([P, NT], F32)
         wb_cols = keep.tile([P, 2 * BLOCKS], F32)
         unit_re = [keep.tile([P, D], F32, name="cr%d" % i) for i in range(NT)]
-        unit_im_neg = [keep.tile([P, D], F32, name="nci%d" % i) for i in range(NT)]
+        unit_im_neg = [keep.tile([P, D], F32, name="nci%d" % i, align_bytes=64) for i in range(NT)]
 
         w_ps = cpsum.tile([P, D], BF16)
         b_ps = cpsum.tile([P, D], BF16)
+
+        ahead = ctx.enter_context(tc.tile_pool(name="ahead", bufs=2))
+        apsum = ctx.enter_context(tc.psum_pool(name="apsum", bufs=2))
+        p0 = {}
+        sine = {}
+
+        def product(i):
+            p0[i] = [apsum.tile([P, BANK], F32, name="p0_%d" % n, tag="p0_%d" % n) for n in range(2)]
+            for n in range(2):
+                for g in range(PASSES):
+                    nc.tensor.matmul_mx(
+                        out=p0[i][n][:],
+                        lhsT=x_codes[:, i, g * P : (g + 1) * P].bitcast(FP8X4),
+                        lhsT_scale=x_scales[:, i, g * P : (g + 1) * P],
+                        rhs=p_codes[:, g, n * BANK : (n + 1) * BANK].bitcast(FP8X4),
+                        rhs_scale=p_scales[:, g, n * BANK : (n + 1) * BANK],
+                        start=(g == 0),
+                        stop=(g == PASSES - 1),
+                    )
+
+        def reduce_range(i):
+            g_i = gain[:, i : i + 1]
+            nearest = ahead.tile([P, D], I32, name="ki", tag="ki", bufs=1)
+            sine[i] = ahead.tile([P, D], F32, name="vs", tag="vs")
+            for n in range(2):
+                cols = slice(n * BANK, (n + 1) * BANK)
+                nc.vector.tensor_scalar(
+                    out=nearest[:, cols], in0=p0[i][n][:], scalar1=g_i, scalar2=None, op0=ALU.mult
+                )
+            for n in range(2):
+                cols = slice(n * BANK, (n + 1) * BANK)
+                nc.vector.scalar_tensor_tensor(
+                    out=sine[i][:, cols], in0=p0[i][n][:], scalar=g_i, in1=nearest[:, cols], op0=ALU.mult,
+                    op1=ALU.subtract,
+                )
+
+        def gains(first, end):
+            sc = sum_cos[:, first:end]
+            ss = sum_sin[:, first:end]
+            nc.vector.tensor_tensor(out=sc, in0=sc, in1=sc, op=ALU.mult)
+            nc.vector.tensor_tensor(out=ss, in0=ss, in1=ss, op=ALU.mult)
+            nc.vector.tensor_tensor(out=sc, in0=sc, in1=ss, op=ALU.add)
+            nc.vector.tensor_scalar(
+                out=gain[:, first:end], in0=sc, scalar1=cf_slope[:, 0:1], scalar2=cf_turns[:, 0:1], op0=ALU.mult,
+                op1=ALU.add,
+            )
 
         with tc.tile_pool(name="stage", bufs=1) as stage, tc.tile_pool(name="xin", bufs=3) as xin, tc.tile_pool(
             name="worka", bufs=2
         ) as worka, tc.psum_pool(name="tpsum", bufs=2) as tpsum:
             rows = stage.tile([P, 2 * D], BF16)
-            nc.vector.memset(rows[:], 0.0)
-            nc.scalar.dma_start(out=rows[0:1, 0:D], in_=ln_weight.rearrange("(o d) -> o d", o=1))
-            nc.scalar.dma_start(out=rows[0:1, D : 2 * D], in_=ln_bias.rearrange("(o d) -> o d", o=1))
+            nc.gpsimd.memset(rows[:], 0.0)
             ones = stage.tile([P, P], BF16)
-            nc.vector.memset(ones[:], 1.0)
-            for h in range(2):
-                nc.tensor.matmul(
-                    out=w_ps[:, h * BANK : (h + 1) * BANK],
-                    lhsT=ones[:],
-                    rhs=rows[:, h * BANK : (h + 1) * BANK],
-                    start=True,
-                    stop=True,
-                )
-            for h in range(2):
-                nc.tensor.matmul(
-                    out=b_ps[:, h * BANK : (h + 1) * BANK],
-                    lhsT=ones[:],
-                    rhs=rows[:, D + h * BANK : D + (h + 1) * BANK],
-                    start=True,
-                    stop=True,
-                )
-
+            nc.gpsimd.memset(ones[:], 1.0)
             wb = stage.tile([P, P], BF16)
-            nc.vector.memset(wb[:], 0.0)
-            nc.scalar.dma_start(out=wb[0:BLOCKS, :], in_=ln_weight.rearrange("(j p) -> j p", p=P))
-            nc.scalar.dma_start(out=wb[BLOCKS : 2 * BLOCKS, :], in_=ln_bias.rearrange("(j p) -> j p", p=P))
+            nc.gpsimd.memset(wb[:], 0.0)
             wb32 = stage.tile([P, P], F32)
-            nc.vector.tensor_copy(out=wb32[:], in_=wb[:])
-            wbt_ps = tpsum.tile([P, BANK], F32, tag="xt")
-            nc.tensor.transpose(out=wbt_ps[:, 0:P], in_=wb32[:], identity=ident[:])
-            nc.vector.tensor_copy(out=wb_cols[:], in_=wbt_ps[:, 0 : 2 * BLOCKS])
+
+            def load_constants():
+                with nc.allow_non_contiguous_dma(reason="one bfloat16 scalar to every partition"):
+                    nc.sync.dma_start(out=cf_bf[:], in_=coherence_factor.partition_broadcast(P))
+                nc.sync.dma_start(out=rows[0:1, 0:D], in_=ln_weight.rearrange("(o d) -> o d", o=1))
+                nc.sync.dma_start(out=rows[0:1, D : 2 * D], in_=ln_bias.rearrange("(o d) -> o d", o=1))
+                nc.sync.dma_start(out=wb[0:BLOCKS, :], in_=ln_weight.rearrange("(j p) -> j p", p=P))
+                nc.sync.dma_start(out=wb[BLOCKS : 2 * BLOCKS, :], in_=ln_bias.rearrange("(j p) -> j p", p=P))
+
+            def spread_constants():
+                nc.vector.tensor_copy(out=cf[:], in_=cf_bf[:])
+                nc.vector.tensor_scalar(
+                    out=cf_turns[:], in0=cf[:], scalar1=1.0 / (2.0 * math.pi), scalar2=None, op0=ALU.mult
+                )
+                nc.vector.tensor_scalar(
+                    out=cf_slope[:], in0=cf[:], scalar1=-1.0 / (2.0 * math.pi * D * D), scalar2=None, op0=ALU.mult
+                )
+                for h in range(2):
+                    nc.tensor.matmul(
+                        out=w_ps[:, h * BANK : (h + 1) * BANK],
+                        lhsT=ones[:],
+                        rhs=rows[:, h * BANK : (h + 1) * BANK],
+                        start=True,
+                        stop=True,
+                    )
+                for h in range(2):
+                    nc.tensor.matmul(
+                        out=b_ps[:, h * BANK : (h + 1) * BANK],
+                        lhsT=ones[:],
+                        rhs=rows[:, D + h * BANK : D + (h + 1) * BANK],
+                        start=True,
+                        stop=True,
+                    )
+                nc.vector.tensor_copy(out=wb32[:], in_=wb[:])
+                wbt_ps = tpsum.tile([P, BANK], F32, name="wbt", tag="xt")
+                nc.tensor.transpose(out=wbt_ps[:, 0:P], in_=wb32[:], identity=ident[:])
+                nc.vector.tensor_copy(out=wb_cols[:], in_=wbt_ps[:, 0 : 2 * BLOCKS])
 
             for i in range(NT):
                 xr = xin.tile([P, D], BF16, tag="xr")
@@ -108,22 +168,28 @@ def tile_quantumcoherencelayer_kernel(
                 nc.sync.dma_start(out=xi[:], in_=xi_d[i])
 
                 if i == 1:
-                    for g in range(PASSES):
-                        raw = stage.tile([P, 4, D], BF16, tag="raw")
+                    for c in range(4):
+                        g, h = divmod(c, 2)
+                        raw = unit_re[NT - 4 + c][:].bitcast(BF16)
                         nc.sync.dma_start(
-                            out=raw[:],
-                            in_=phase_matrix[512 * g : 512 * (g + 1), :].rearrange("(q t) c -> q t c", t=4),
+                            out=raw.rearrange("p (t c) -> p t c", t=4),
+                            in_=phase_matrix[512 * g : 512 * (g + 1), BANK * h : BANK * (h + 1)].rearrange(
+                                "(q t) c -> q t c", t=4
+                            ),
                         )
-                        pg = stage.tile([P, D, 4], BF16, tag="pg", align_bytes=64)
+                        pg = unit_im_neg[NT - 4 + c][:].bitcast(BF16)
                         nc.vector.tensor_copy(
-                            out=pg[:].rearrange("p (c i) t -> p c t i", i=4),
-                            in_=raw[:].rearrange("p t (c i) -> p c t i", i=4),
+                            out=pg.rearrange("p (c i t) -> p c t i", i=4, t=4),
+                            in_=raw.rearrange("p (t c i) -> p c t i", t=4, i=4),
                         )
                         nc.vector.quantize_mx(
-                            out=p_codes[:, g, :].bitcast(FP8X4),
-                            scales=p_scales[:, g, :],
-                            in_=pg[:].rearrange("p c t -> p (c t)"),
+                            out=p_codes[:, g, BANK * h : BANK * (h + 1)].bitcast(FP8X4),
+                            scales=p_scales[:, g, BANK * h : BANK * (h + 1)],
+                            in_=pg,
                         )
+                    load_constants()
+                if i == 3:
+                    spread_constants()
 
                 xt = tpsum.tile([P, BANK], F32, tag="xt")
                 xw = xr[:].bitcast(F32)
@@ -157,6 +223,11 @@ def tile_quantumcoherencelayer_kernel(
                 nc.scalar.activation(
                     out=inv_n[:], in_=inv_n[:], func=ACT.Abs_reciprocal_sqrt, bias=eps_t[:, 0:1], scale=1.0
                 )
+                if i == NT - 1:
+                    gains(0, AHEAD)
+                    for j in range(AHEAD):
+                        product(j)
+                        reduce_range(j)
                 nc.vector.scalar_tensor_tensor(
                     out=scr_a[:], in0=xr[:], scalar=EPS, in1=inv_r[:], op0=ALU.add, op1=ALU.mult,
                     accum_out=sum_cos[:, i : i + 1],
@@ -170,22 +241,11 @@ def tile_quantumcoherencelayer_kernel(
                     out=unit_im_neg[i][:], in0=xi[:], scalar=-1.0, in1=inv_n[:], op0=ALU.mult, op1=ALU.mult
                 )
 
-            nc.vector.tensor_tensor(out=sum_cos[:], in0=sum_cos[:], in1=sum_cos[:], op=ALU.mult)
-            nc.vector.tensor_tensor(out=sum_sin[:], in0=sum_sin[:], in1=sum_sin[:], op=ALU.mult)
-            nc.vector.tensor_tensor(out=sum_cos[:], in0=sum_cos[:], in1=sum_sin[:], op=ALU.add)
-            nc.vector.tensor_scalar(
-                out=sum_cos[:], in0=sum_cos[:], scalar1=-1.0 / (D * D), scalar2=1.0, op0=ALU.mult, op1=ALU.add
-            )
-            nc.vector.tensor_scalar(
-                out=gain[:], in0=sum_cos[:], scalar1=cf[:, 0:1], scalar2=1.0 / (2.0 * math.pi), op0=ALU.mult,
-                op1=ALU.mult,
-            )
+            gains(AHEAD, NT)
 
         with tc.tile_pool(name="workb", bufs=2) as workb, tc.tile_pool(name="stat", bufs=4) as stat, tc.psum_pool(
             name="ppsum", bufs=2
         ) as ppsum, tc.manual_schedule():
-            p0 = {}
-            sine = {}
             vers = {}
             out_re = {}
             cos_im = {}
@@ -204,38 +264,8 @@ def tile_quantumcoherencelayer_kernel(
             def turned(i):
                 return 0 <= i < NT - 1
 
-            def product(i):
-                p0[i] = [ppsum.tile([P, BANK], F32, name="p0_%d" % n, tag="p0_%d" % n) for n in range(2)]
-                for n in range(2):
-                    for g in range(PASSES):
-                        nc.tensor.matmul_mx(
-                            out=p0[i][n][:],
-                            lhsT=x_codes[:, i, g * P : (g + 1) * P].bitcast(FP8X4),
-                            lhsT_scale=x_scales[:, i, g * P : (g + 1) * P],
-                            rhs=p_codes[:, g, n * BANK : (n + 1) * BANK].bitcast(FP8X4),
-                            rhs_scale=p_scales[:, g, n * BANK : (n + 1) * BANK],
-                            start=(g == 0),
-                            stop=(g == PASSES - 1),
-                        )
-
-            def reduce_range(i):
-                g_i = gain[:, i : i + 1]
-                nearest = workb.tile([P, D], I32, name="ki", tag="ki", bufs=1)
-                sine[i] = workb.tile([P, D], F32, name="vs", tag="vs")
-                for n in range(2):
-                    cols = slice(n * BANK, (n + 1) * BANK)
-                    nc.vector.tensor_scalar(
-                        out=nearest[:, cols], in0=p0[i][n][:], scalar1=g_i, scalar2=None, op0=ALU.mult
-                    )
-                for n in range(2):
-                    cols = slice(n * BANK, (n + 1) * BANK)
-                    nc.vector.scalar_tensor_tensor(
-                        out=sine[i][:, cols], in0=p0[i][n][:], scalar=g_i, in1=nearest[:, cols], op0=ALU.mult,
-                        op1=ALU.subtract,
-                    )
-
             def two_sines(i):
-                vers[i] = workb.tile([P, D], F32, name="hh", tag="hh")
+                vers[i] = ahead.tile([P, D], F32, name="hh", tag="hh")
                 nc.scalar.activation(out=vers[i][:], in_=sine[i][:], func=ACT.Sin, scale=math.pi)
                 nc.scalar.activation(out=sine[i][:], in_=sine[i][:], func=ACT.Sin, scale=2.0 * math.pi)
 
@@ -336,7 +366,7 @@ def tile_quantumcoherencelayer_kernel(
                     nc.tensor.transpose(out=t2[:, jj * P : (jj + 1) * P], in_=turned_im[i][:, j, :], identity=ident[:])
                 nc.scalar.copy(out=rot_im[i][:, half * BANK : (half + 1) * BANK], in_=t2[:])
 
-            for k in range(-3, NT + 1):
+            for k in range(-1, NT + 1):
                 if valid(k + 1):
                     two_sines(k + 1)
                 if turned(k - 2):
@@ -355,7 +385,7 @@ def tile_quantumcoherencelayer_kernel(
                 if turned(k - 1):
                     turned_im[k - 1] = workb.tile([P, BLOCKS, P], F32, name="ot", tag="ot", bufs=1)
                     there(k - 1, 0)
-                if valid(k + 3):
+                if AHEAD <= k + 3 < NT:
                     product(k + 3)
                 if valid(k):
                     variances(k)
@@ -372,5 +402,5 @@ def tile_quantumcoherencelayer_kernel(
                     sine_products_on_gpsimd(k + 1)
                 if valid(k):
                     inverse_deviations(k)
-                if valid(k + 2):
+                if AHEAD <= k + 2 < NT:
                     reduce_range(k + 2)

@@ -70,6 +70,7 @@ def tile_quantumcoherencelayer_kernel(
         ahead = ctx.enter_context(tc.tile_pool(name="ahead", bufs=2))
         apsum = ctx.enter_context(tc.psum_pool(name="apsum", bufs=2))
         p0 = {}
+        nearest = {}
         sine = {}
 
         def product(i):
@@ -86,20 +87,21 @@ def tile_quantumcoherencelayer_kernel(
                         stop=(g == PASSES - 1),
                     )
 
-        def reduce_range(i):
-            g_i = gain[:, i : i + 1]
-            nearest = ahead.tile([P, D], I32, name="ki", tag="ki", bufs=1)
-            sine[i] = ahead.tile([P, D], F32, name="vs", tag="vs")
+        def nearest_turns(i):
+            nearest[i] = ahead.tile([P, D], I32, name="ki", tag="ki", bufs=1)
             for n in range(2):
                 cols = slice(n * BANK, (n + 1) * BANK)
                 nc.vector.tensor_scalar(
-                    out=nearest[:, cols], in0=p0[i][n][:], scalar1=g_i, scalar2=None, op0=ALU.mult
+                    out=nearest[i][:, cols], in0=p0[i][n][:], scalar1=gain[:, i : i + 1], scalar2=None, op0=ALU.mult
                 )
+
+        def reduced_angle(i):
+            sine[i] = ahead.tile([P, D], F32, name="vs", tag="vs")
             for n in range(2):
                 cols = slice(n * BANK, (n + 1) * BANK)
                 nc.vector.scalar_tensor_tensor(
-                    out=sine[i][:, cols], in0=p0[i][n][:], scalar=g_i, in1=nearest[:, cols], op0=ALU.mult,
-                    op1=ALU.subtract,
+                    out=sine[i][:, cols], in0=p0[i][n][:], scalar=gain[:, i : i + 1], in1=nearest[i][:, cols],
+                    op0=ALU.mult, op1=ALU.subtract,
                 )
 
         def gains(first, end):
@@ -227,7 +229,8 @@ def tile_quantumcoherencelayer_kernel(
                     gains(0, AHEAD)
                     for j in range(AHEAD):
                         product(j)
-                        reduce_range(j)
+                        nearest_turns(j)
+                        reduced_angle(j)
                 nc.vector.scalar_tensor_tensor(
                     out=scr_a[:], in0=xr[:], scalar=EPS, in1=inv_r[:], op0=ALU.add, op1=ALU.mult,
                     accum_out=sum_cos[:, i : i + 1],
@@ -300,17 +303,15 @@ def tile_quantumcoherencelayer_kernel(
                     op0=ALU.add, op1=ALU.mult,
                 )
 
-            def imaginary_part_and_means(i):
+            def imaginary_part(i):
                 nc.vector.scalar_tensor_tensor(
                     out=rot_im[i][:], in0=rot_im[i][:], scalar=1.0, in1=cos_im[i][:], op0=ALU.mult, op1=ALU.add,
                     accum_out=sums[i][:, 1:2],
                 )
-                neg_mean[i] = stat.tile([P, 2], F32, name="nmu", tag="nmu")
-                nc.vector.tensor_scalar(
-                    out=neg_mean[i][:], in0=sums[i][:], scalar1=-1.0 / D, scalar2=None, op0=ALU.mult
-                )
 
             def variances(i):
+                neg_mean[i] = stat.tile([P, 2], F32, name="nmu", tag="nmu")
+                nc.scalar.activation(out=neg_mean[i][:], in_=sums[i][:], func=ACT.Identity, scale=-1.0 / D)
                 sq_dev[i] = stat.tile([P, 2], F32, name="sq", tag="sq")
                 nc.scalar.activation(
                     out=vers[i][:], in_=rot_re[i][:], func=ACT.Square, bias=neg_mean[i][:, 0:1], scale=1.0,
@@ -337,10 +338,12 @@ def tile_quantumcoherencelayer_kernel(
                 inv_std[i] = stat.tile([P, 2], F32, name="rstd", tag="rstd")
                 nc.gpsimd.tensor_tensor(out=inv_std[i][:], in0=var_eps[i][:], in1=neghalf[:], op=ALU.pow)
 
-            def scale_shift(dst, src, i, c):
+            def scale(dst, src, i, c):
                 nc.vector.scalar_tensor_tensor(
                     out=dst[:], in0=src[:], scalar=neg_mean[i][:, c : c + 1], in1=w_ps[:], op0=ALU.add, op1=ALU.mult
                 )
+
+            def shift(dst, i, c):
                 nc.vector.scalar_tensor_tensor(
                     out=dst[:], in0=dst[:], scalar=inv_std[i][:, c : c + 1], in1=b_ps[:], op0=ALU.mult, op1=ALU.add
                 )
@@ -379,7 +382,7 @@ def tile_quantumcoherencelayer_kernel(
                 if turned(k - 1):
                     normalise_im(k - 1)
                 if valid(k):
-                    imaginary_part_and_means(k)
+                    imaginary_part(k)
                 if valid(k + 1):
                     versine(k + 1)
                 if turned(k - 1):
@@ -393,14 +396,20 @@ def tile_quantumcoherencelayer_kernel(
                     back(k - 1, 0)
                     there(k - 1, 1)
                 if valid(k - 1):
-                    scale_shift(out_re[k - 1], rot_re[k - 1], k - 1, 0)
+                    scale(out_re[k - 1], rot_re[k - 1], k - 1, 0)
+                if k - 1 == NT - 1:
+                    scale(rot_im[k - 1], rot_im[k - 1], k - 1, 1)
+                if AHEAD <= k + 2 < NT:
+                    nearest_turns(k + 2)
+                if valid(k - 1):
+                    shift(out_re[k - 1], k - 1, 0)
                     nc.sync.dma_start(out=o0_d[k - 1], in_=out_re[k - 1][:])
                 if k - 1 == NT - 1:
-                    scale_shift(rot_im[k - 1], rot_im[k - 1], k - 1, 1)
+                    shift(rot_im[k - 1], k - 1, 1)
                     nc.sync.dma_start(out=o1_d[k - 1], in_=rot_im[k - 1][:])
                 if valid(k + 1):
                     sine_products_on_gpsimd(k + 1)
                 if valid(k):
                     inverse_deviations(k)
                 if AHEAD <= k + 2 < NT:
-                    reduce_range(k + 2)
+                    reduced_angle(k + 2)

@@ -21,7 +21,7 @@ BANK = 512
 PASSES = D // 512
 BLOCKS = D // P
 EPS = 1e-8
-POOL_COLS = 896
+POOL_COLS = 640
 AHEAD = 2
 FLOPS = 2 * ROWS * D * D
 

@@ -21,7 +21,7 @@ BANK = 512
 PASSES = D // 512
 BLOCKS = D // P
 EPS = 1e-8
-POOL_COLS = 640
+POOL_COLS = 704
 AHEAD = 2
 FLOPS = 2 * ROWS * D * D
 

@@ -37,7 +37,6 @@ def tile_quantumcoherencelayer_kernel(
 
     with ExitStack() as ctx:
         keep = ctx.enter_context(tc.tile_pool(name="keep", bufs=1))
-        cpsum = ctx.enter_context(tc.psum_pool(name="cpsum", bufs=1))
 
         ident = keep.tile([P, P], F32)
         make_identity(nc, ident[:])
@@ -57,24 +56,23 @@ def tile_quantumcoherencelayer_kernel(
         p_scales = keep.tile([P, PASSES, D], U8, align_bytes=64)
         x_codes = keep.tile([P, NT, PASSES * P], U32, align_bytes=64)
         x_scales = keep.tile([P, NT, PASSES * P], U8, align_bytes=64)
-        sum_cos = keep.tile([P, NT], F32)
-        sum_sin = keep.tile([P, NT], F32)
+        coh = keep.tile([P, 2, 2, NT], F32)
         gain = keep.tile([P, NT], F32)
         wb_cols = keep.tile([P, 2 * BLOCKS], F32)
         unit_re = [keep.tile([P, D], F32, name="cr%d" % i) for i in range(NT)]
         unit_im_neg = [keep.tile([P, D], F32, name="nci%d" % i, align_bytes=64) for i in range(NT)]
 
-        w_ps = cpsum.tile([P, D], BF16)
-        b_ps = cpsum.tile([P, D], BF16)
+        rows = keep.tile([P, 2 * D], BF16)
+        ones = keep.tile([P, P], BF16)
 
         ahead = ctx.enter_context(tc.tile_pool(name="ahead", bufs=2))
-        apsum = ctx.enter_context(tc.psum_pool(name="apsum", bufs=2))
+        apsum = ctx.enter_context(tc.psum_pool(name="apsum", bufs=3))
         p0 = {}
         nearest = {}
         sine = {}
 
         def product(i):
-            p0[i] = [apsum.tile([P, BANK], F32, name="p0_%d" % n, tag="p0_%d" % n) for n in range(2)]
+            p0[i] = [apsum.tile([P, BANK], F32, name="p0_%d" % n, tag="bank") for n in range(2)]
             for n in range(2):
                 for g in range(PASSES):
                     nc.tensor.matmul_mx(
@@ -105,26 +103,36 @@ def tile_quantumcoherencelayer_kernel(
                 )
 
         def gains(first, end):
-            sc = sum_cos[:, first:end]
-            ss = sum_sin[:, first:end]
-            nc.vector.tensor_tensor(out=sc, in0=sc, in1=sc, op=ALU.mult)
-            nc.vector.tensor_tensor(out=ss, in0=ss, in1=ss, op=ALU.mult)
-            nc.vector.tensor_tensor(out=sc, in0=sc, in1=ss, op=ALU.add)
+            both = coh[:, 0, :, first:end]
+            nc.vector.tensor_tensor(out=both, in0=both, in1=coh[:, 1, :, first:end], op=ALU.add)
+            nc.vector.tensor_tensor(out=both, in0=both, in1=both, op=ALU.mult)
+            nc.vector.tensor_tensor(
+                out=coh[:, 0, 0, first:end], in0=coh[:, 0, 0, first:end], in1=coh[:, 0, 1, first:end], op=ALU.add
+            )
             nc.vector.tensor_scalar(
-                out=gain[:, first:end], in0=sc, scalar1=cf_slope[:, 0:1], scalar2=cf_turns[:, 0:1], op0=ALU.mult,
-                op1=ALU.add,
+                out=gain[:, first:end], in0=coh[:, 0, 0, first:end], scalar1=cf_slope[:, 0:1], scalar2=cf_turns[:, 0:1],
+                op0=ALU.mult, op1=ALU.add,
             )
 
-        with tc.tile_pool(name="stage", bufs=1) as stage, tc.tile_pool(name="xin", bufs=3) as xin, tc.tile_pool(
+        nc.gpsimd.memset(rows[:], 0.0)
+        nc.gpsimd.memset(ones[:], 1.0)
+        with tc.tile_pool(name="stage", bufs=1) as stage, tc.tile_pool(name="xin", bufs=5) as xin, tc.tile_pool(
             name="worka", bufs=2
-        ) as worka, tc.psum_pool(name="tpsum", bufs=2) as tpsum:
-            rows = stage.tile([P, 2 * D], BF16)
-            nc.gpsimd.memset(rows[:], 0.0)
-            ones = stage.tile([P, P], BF16)
-            nc.gpsimd.memset(ones[:], 1.0)
+        ) as worka, tc.psum_pool(name="tpsum", bufs=1) as tpsum, tc.manual_schedule():
             wb = stage.tile([P, P], BF16)
             nc.gpsimd.memset(wb[:], 0.0)
             wb32 = stage.tile([P, P], F32)
+            xr = {}
+            xi = {}
+            sq_re_eps = {}
+            sq_im_eps = {}
+            sq_re = {}
+            sq_im = {}
+            summed = {}
+            inv = {}
+            inv_rows = {}
+            words = {}
+            grouped = {}
 
             def load_constants():
                 with nc.allow_non_contiguous_dma(reason="one bfloat16 scalar to every partition"):
@@ -134,121 +142,184 @@ def tile_quantumcoherencelayer_kernel(
                 nc.sync.dma_start(out=wb[0:BLOCKS, :], in_=ln_weight.rearrange("(j p) -> j p", p=P))
                 nc.sync.dma_start(out=wb[BLOCKS : 2 * BLOCKS, :], in_=ln_bias.rearrange("(j p) -> j p", p=P))
 
-            def spread_constants():
-                nc.vector.tensor_copy(out=cf[:], in_=cf_bf[:])
-                nc.vector.tensor_scalar(
-                    out=cf_turns[:], in0=cf[:], scalar1=1.0 / (2.0 * math.pi), scalar2=None, op0=ALU.mult
+            def load(i):
+                xr[i] = xin.tile([P, D], BF16, name="xr", tag="xr")
+                nc.sync.dma_start(out=xr[i][:], in_=xr_d[i])
+                xi[i] = xin.tile([P, D], BF16, name="xi", tag="xi")
+                nc.sync.dma_start(out=xi[i][:], in_=xi_d[i])
+
+            def square_re_eps(i):
+                sq_re_eps[i] = ahead.tile([P, D], F32, name="vs", tag="vs")
+                nc.scalar.activation(out=sq_re_eps[i][:], in_=xr[i][:], func=ACT.Square, bias=eps_t[:, 0:1], scale=1.0)
+
+            def square_im_eps(i):
+                sq_im_eps[i] = ahead.tile([P, D], F32, name="hh", tag="hh")
+                nc.scalar.activation(out=sq_im_eps[i][:], in_=xi[i][:], func=ACT.Square, bias=eps_t[:, 0:1], scale=1.0)
+
+            def squares(i):
+                sq_re[i] = worka.tile([P, D], F32, name="sr", tag="sr")
+                nc.gpsimd.tensor_tensor(out=sq_re[i][:], in0=xr[i][:], in1=xr[i][:], op=ALU.mult)
+                sq_im[i] = worka.tile([P, D], F32, name="si", tag="si")
+                nc.gpsimd.tensor_tensor(out=sq_im[i][:], in0=xi[i][:], in1=xi[i][:], op=ALU.mult)
+
+            def flip_sum(key, a, b, h):
+                summed[key] = apsum.tile([P, BANK], F32, name="sum", tag="bank")
+                for jj in range(4):
+                    cols = slice(h * BANK + jj * P, h * BANK + (jj + 1) * P)
+                    for src, first in ((a, True), (b, False)):
+                        nc.tensor.matmul(
+                            out=summed[key][:, jj * P : (jj + 1) * P], lhsT=src[:, cols], rhs=ident[:], start=first,
+                            stop=not first, is_transpose=True,
+                        )
+
+            def inverse_r(key):
+                inv[key] = worka.tile([P, BANK], F32, name="ir", tag="ir")
+                nc.scalar.activation(out=inv[key][:], in_=summed[key][:], func=ACT.Abs_reciprocal_sqrt)
+
+            def inverse_n(key):
+                inv[key] = worka.tile([P, BANK], F32, name="in", tag="in")
+                nc.scalar.activation(
+                    out=inv[key][:], in_=summed[key][:], func=ACT.Abs_reciprocal_sqrt, bias=eps_t[:, 0:1], scale=1.0
                 )
-                nc.vector.tensor_scalar(
-                    out=cf_slope[:], in0=cf[:], scalar1=-1.0 / (2.0 * math.pi * D * D), scalar2=None, op0=ALU.mult
-                )
-                for h in range(2):
-                    nc.tensor.matmul(
-                        out=w_ps[:, h * BANK : (h + 1) * BANK],
-                        lhsT=ones[:],
-                        rhs=rows[:, h * BANK : (h + 1) * BANK],
-                        start=True,
-                        stop=True,
+
+            def flip_back(key):
+                inv_rows[key] = tpsum.tile([P, BANK], F32, name="bk", tag="bk", bufs=4)
+                for jj in range(4):
+                    nc.tensor.transpose(
+                        out=inv_rows[key][:, jj * P : (jj + 1) * P], in_=inv[key][:, jj * P : (jj + 1) * P],
+                        identity=ident[:],
                     )
-                for h in range(2):
-                    nc.tensor.matmul(
-                        out=b_ps[:, h * BANK : (h + 1) * BANK],
-                        lhsT=ones[:],
-                        rhs=rows[:, D + h * BANK : D + (h + 1) * BANK],
-                        start=True,
-                        stop=True,
-                    )
-                nc.vector.tensor_copy(out=wb32[:], in_=wb[:])
-                wbt_ps = tpsum.tile([P, BANK], F32, name="wbt", tag="xt")
-                nc.tensor.transpose(out=wbt_ps[:, 0:P], in_=wb32[:], identity=ident[:])
-                nc.vector.tensor_copy(out=wb_cols[:], in_=wbt_ps[:, 0 : 2 * BLOCKS])
 
-            for i in range(NT):
-                xr = xin.tile([P, D], BF16, tag="xr")
-                nc.sync.dma_start(out=xr[:], in_=xr_d[i])
-                xi = xin.tile([P, D], BF16, tag="xi")
-                nc.sync.dma_start(out=xi[:], in_=xi_d[i])
-
-                if i == 1:
-                    for c in range(4):
-                        g, h = divmod(c, 2)
-                        raw = unit_re[NT - 4 + c][:].bitcast(BF16)
-                        nc.sync.dma_start(
-                            out=raw.rearrange("p (t c) -> p t c", t=4),
-                            in_=phase_matrix[512 * g : 512 * (g + 1), BANK * h : BANK * (h + 1)].rearrange(
-                                "(q t) c -> q t c", t=4
-                            ),
-                        )
-                        pg = unit_im_neg[NT - 4 + c][:].bitcast(BF16)
-                        nc.vector.tensor_copy(
-                            out=pg.rearrange("p (c i t) -> p c t i", i=4, t=4),
-                            in_=raw.rearrange("p (t c i) -> p c t i", t=4, i=4),
-                        )
-                        nc.vector.quantize_mx(
-                            out=p_codes[:, g, BANK * h : BANK * (h + 1)].bitcast(FP8X4),
-                            scales=p_scales[:, g, BANK * h : BANK * (h + 1)],
-                            in_=pg,
-                        )
-                    load_constants()
-                if i == 3:
-                    spread_constants()
-
-                xt = tpsum.tile([P, BANK], F32, tag="xt")
-                xw = xr[:].bitcast(F32)
+            def transpose_words(i):
+                words[i] = tpsum.tile([P, BANK], F32, name="xt", tag="xt")
+                xw = xr[i][:].bitcast(F32)
                 for j in range(4):
                     g, u = divmod(j, 2)
                     nc.tensor.transpose(
-                        out=xt[:, j * P : (j + 1) * P], in_=xw[:, 256 * g + u : 256 * (g + 1) : 2], identity=ident[:]
+                        out=words[i][:, j * P : (j + 1) * P], in_=xw[:, 256 * g + u : 256 * (g + 1) : 2],
+                        identity=ident[:],
                     )
-                grouped = worka.tile([P, PASSES, P, 4], BF16, tag="grouped", align_bytes=64)
+
+            def group_words(i):
+                if i % 2 == 0:
+                    grouped[i // 2] = worka.tile(
+                        [P, 2, PASSES, P, 4], BF16, name="grouped", tag="grouped", align_bytes=64
+                    )
                 nc.scalar.copy(
-                    out=grouped[:].bitcast(F32),
-                    in_=xt[:].rearrange("p (g u r) -> p g r u", g=PASSES, u=2),
+                    out=grouped[i // 2][:, i % 2].bitcast(F32),
+                    in_=words[i][:].rearrange("p (g u r) -> p g r u", g=PASSES, u=2),
                 )
 
-                inv_r = worka.tile([P, D], F32, tag="sa")
-                scr_a = worka.tile([P, D], F32, tag="sb")
-                inv_n = worka.tile([P, D], F32, tag="sr")
-                scr_b = worka.tile([P, D], F32, tag="si")
-                nc.scalar.activation(out=inv_r[:], in_=xr[:], func=ACT.Square, bias=eps_t[:, 0:1], scale=1.0)
-                nc.scalar.activation(out=scr_a[:], in_=xi[:], func=ACT.Square, bias=eps_t[:, 0:1], scale=1.0)
-                nc.scalar.activation(out=inv_n[:], in_=xr[:], func=ACT.Square)
-                nc.scalar.activation(out=scr_b[:], in_=xi[:], func=ACT.Square)
-                nc.vector.tensor_tensor(out=inv_r[:], in0=inv_r[:], in1=scr_a[:], op=ALU.add)
-                nc.vector.tensor_tensor(out=inv_n[:], in0=inv_n[:], in1=scr_b[:], op=ALU.add)
+            def quantize_pair(j):
                 nc.vector.quantize_mx(
-                    out=x_codes[:, i, :].bitcast(FP8X4),
-                    scales=x_scales[:, i, :],
-                    in_=grouped[:].rearrange("p g r t -> p (g r t)"),
+                    out=x_codes[:, 2 * j : 2 * j + 2, :].rearrange("p i c -> p (i c)").bitcast(FP8X4),
+                    scales=x_scales[:, 2 * j : 2 * j + 2, :].rearrange("p i c -> p (i c)"),
+                    in_=grouped[j][:].rearrange("p i g r t -> p (i g r t)"),
                 )
-                nc.scalar.activation(out=inv_r[:], in_=inv_r[:], func=ACT.Abs_reciprocal_sqrt)
-                nc.scalar.activation(
-                    out=inv_n[:], in_=inv_n[:], func=ACT.Abs_reciprocal_sqrt, bias=eps_t[:, 0:1], scale=1.0
+
+            def vector_half(i, h):
+                cols = slice(h * BANK, (h + 1) * BANK)
+                for src, junk, c in ((xr, unit_im_neg, 0), (xi, unit_re, 1)):
+                    nc.vector.scalar_tensor_tensor(
+                        out=junk[i][:, cols], in0=src[i][:, cols], scalar=EPS, in1=inv_rows[("r", i, h)][:], op0=ALU.add,
+                        op1=ALU.mult, accum_out=coh[:, h, c, i : i + 1],
+                    )
+                nc.vector.scalar_tensor_tensor(
+                    out=unit_im_neg[i][:, cols], in0=xi[i][:, cols], scalar=-1.0, in1=inv_rows[("n", i, h)][:],
+                    op0=ALU.mult, op1=ALU.mult,
                 )
-                if i == NT - 1:
+                nc.vector.tensor_tensor(
+                    out=unit_re[i][:, cols], in0=xr[i][:, cols], in1=inv_rows[("n", i, h)][:], op=ALU.mult
+                )
+
+            load(0)
+            load(1)
+            for c in range(4):
+                g, h = divmod(c, 2)
+                raw = unit_re[NT - 4 + c][:].bitcast(BF16)
+                nc.sync.dma_start(
+                    out=raw.rearrange("p (t c) -> p t c", t=4),
+                    in_=phase_matrix[512 * g : 512 * (g + 1), BANK * h : BANK * (h + 1)].rearrange(
+                        "(q t) c -> q t c", t=4
+                    ),
+                )
+                pg = unit_im_neg[NT - 4 + c][:].bitcast(BF16)
+                nc.vector.tensor_copy(
+                    out=pg.rearrange("p (c i t) -> p c t i", i=4, t=4),
+                    in_=raw.rearrange("p (t c i) -> p c t i", t=4, i=4),
+                )
+                nc.vector.quantize_mx(
+                    out=p_codes[:, g, BANK * h : BANK * (h + 1)].bitcast(FP8X4),
+                    scales=p_scales[:, g, BANK * h : BANK * (h + 1)],
+                    in_=pg,
+                )
+            load_constants()
+
+            for k in range(-2, NT):
+                s, f = k + 2, k + 1
+                if k + 4 < NT:
+                    load(k + 4)
+                if s < NT:
+                    square_re_eps(s)
+                    squares(s)
+                if 0 <= f < NT:
+                    flip_sum(("r", f, 0), sq_re_eps[f], sq_im_eps[f], 0)
+                    inverse_r(("r", f, 0))
+                    flip_sum(("n", f, 0), sq_re[f], sq_im[f], 0)
+                    inverse_n(("n", f, 0))
+                    flip_sum(("r", f, 1), sq_re_eps[f], sq_im_eps[f], 1)
+                if s < NT:
+                    square_im_eps(s)
+                    transpose_words(s)
+                if 0 <= f < NT:
+                    inverse_r(("r", f, 1))
+                    flip_back(("r", f, 0))
+                    flip_back(("n", f, 0))
+                    flip_sum(("n", f, 1), sq_re[f], sq_im[f], 1)
+                    inverse_n(("n", f, 1))
+                if s < NT:
+                    group_words(s)
+                if 0 <= f < NT:
+                    flip_back(("r", f, 1))
+                    flip_back(("n", f, 1))
+                if k == 2:
+                    nc.vector.tensor_copy(out=cf[:], in_=cf_bf[:])
+                    nc.vector.tensor_scalar(
+                        out=cf_turns[:], in0=cf[:], scalar1=1.0 / (2.0 * math.pi), scalar2=None, op0=ALU.mult
+                    )
+                    nc.vector.tensor_scalar(
+                        out=cf_slope[:], in0=cf[:], scalar1=-1.0 / (2.0 * math.pi * D * D), scalar2=None, op0=ALU.mult
+                    )
+                    nc.vector.tensor_copy(out=wb32[:], in_=wb[:])
+                    wbt_ps = apsum.tile([P, BANK], F32, name="wbt", tag="bank")
+                    nc.tensor.transpose(out=wbt_ps[:, 0:P], in_=wb32[:], identity=ident[:])
+                if k == 3:
+                    nc.vector.tensor_copy(out=wb_cols[:], in_=wbt_ps[:, 0 : 2 * BLOCKS])
+                if k == NT - 1:
                     gains(0, AHEAD)
                     for j in range(AHEAD):
                         product(j)
                         nearest_turns(j)
                         reduced_angle(j)
-                nc.vector.scalar_tensor_tensor(
-                    out=scr_a[:], in0=xr[:], scalar=EPS, in1=inv_r[:], op0=ALU.add, op1=ALU.mult,
-                    accum_out=sum_cos[:, i : i + 1],
-                )
-                nc.vector.scalar_tensor_tensor(
-                    out=scr_b[:], in0=xi[:], scalar=EPS, in1=inv_r[:], op0=ALU.add, op1=ALU.mult,
-                    accum_out=sum_sin[:, i : i + 1],
-                )
-                nc.vector.tensor_tensor(out=unit_re[i][:], in0=xr[:], in1=inv_n[:], op=ALU.mult)
-                nc.vector.scalar_tensor_tensor(
-                    out=unit_im_neg[i][:], in0=xi[:], scalar=-1.0, in1=inv_n[:], op0=ALU.mult, op1=ALU.mult
-                )
+                if k >= 0:
+                    vector_half(k, 0)
+                    if k % 2 == 0:
+                        quantize_pair(k // 2)
+                    vector_half(k, 1)
 
             gains(AHEAD, NT)
 
         with tc.tile_pool(name="workb", bufs=2) as workb, tc.tile_pool(name="stat", bufs=4) as stat, tc.psum_pool(
             name="ppsum", bufs=2
         ) as ppsum, tc.manual_schedule():
+            w_ps = ppsum.tile([P, D], BF16, name="w_ps", tag="w_ps", bufs=1)
+            b_ps = ppsum.tile([P, D], BF16, name="b_ps", tag="b_ps", bufs=1)
+            for dst, at in ((w_ps, 0), (b_ps, D)):
+                for h in range(2):
+                    nc.tensor.matmul(
+                        out=dst[:, h * BANK : (h + 1) * BANK], lhsT=ones[:],
+                        rhs=rows[:, at + h * BANK : at + (h + 1) * BANK], start=True, stop=True,
+                    )
             vers = {}
             out_re = {}
             cos_im = {}
@@ -375,6 +446,8 @@ def tile_quantumcoherencelayer_kernel(
                 if turned(k - 2):
                     back(k - 2, 1)
                     nc.sync.dma_start(out=o1_d[k - 2], in_=rot_im[k - 2][:])
+                if AHEAD <= k + 2 < NT:
+                    product(k + 2)
                 if valid(k):
                     cosine_products_and_real_part(k)
                 if valid(k + 1):
@@ -388,8 +461,6 @@ def tile_quantumcoherencelayer_kernel(
                 if turned(k - 1):
                     turned_im[k - 1] = workb.tile([P, BLOCKS, P], F32, name="ot", tag="ot", bufs=1)
                     there(k - 1, 0)
-                if AHEAD <= k + 3 < NT:
-                    product(k + 3)
                 if valid(k):
                     variances(k)
                 if turned(k - 1):

@@ -22,6 +22,9 @@ PASSES = D // 512
 BLOCKS = D // P
 EPS = 1e-8
 POOL_COLS = 704
+SCALAR_SQUARES = 3
+TURNED = 768
+GPSIMD_COLS = 768
 AHEAD = 2
 FLOPS = 2 * ROWS * D * D
 
@@ -114,11 +117,11 @@ def tile_quantumcoherencelayer_kernel(
                 op0=ALU.mult, op1=ALU.add,
             )
 
-        nc.gpsimd.memset(rows[:], 0.0)
-        nc.gpsimd.memset(ones[:], 1.0)
-        with tc.tile_pool(name="stage", bufs=1) as stage, tc.tile_pool(name="xin", bufs=5) as xin, tc.tile_pool(
+        with tc.tile_pool(name="stage", bufs=1) as stage, tc.tile_pool(name="xin", bufs=4) as xin, tc.tile_pool(
             name="worka", bufs=2
         ) as worka, tc.psum_pool(name="tpsum", bufs=1) as tpsum, tc.manual_schedule():
+            nc.gpsimd.memset(rows[:], 0.0)
+            nc.gpsimd.memset(ones[:], 1.0)
             wb = stage.tile([P, P], BF16)
             nc.gpsimd.memset(wb[:], 0.0)
             wb32 = stage.tile([P, P], F32)
@@ -130,6 +133,7 @@ def tile_quantumcoherencelayer_kernel(
             sq_im = {}
             summed = {}
             inv = {}
+            rest_n = {}
             inv_rows = {}
             words = {}
             grouped = {}
@@ -143,28 +147,36 @@ def tile_quantumcoherencelayer_kernel(
                 nc.sync.dma_start(out=wb[BLOCKS : 2 * BLOCKS, :], in_=ln_bias.rearrange("(j p) -> j p", p=P))
 
             def load(i):
-                xr[i] = xin.tile([P, D], BF16, name="xr", tag="xr")
-                nc.sync.dma_start(out=xr[i][:], in_=xr_d[i])
-                xi[i] = xin.tile([P, D], BF16, name="xi", tag="xi")
-                nc.sync.dma_start(out=xi[i][:], in_=xi_d[i])
+                both = xin.tile([P, 2, D], BF16, name="x", tag="x")
+                xr[i] = both[:, 0, :]
+                xi[i] = both[:, 1, :]
+                nc.sync.dma_start(out=xr[i], in_=xr_d[i])
+                nc.sync.dma_start(out=xi[i], in_=xi_d[i])
 
             def square_re_eps(i):
                 sq_re_eps[i] = ahead.tile([P, D], F32, name="vs", tag="vs")
-                nc.scalar.activation(out=sq_re_eps[i][:], in_=xr[i][:], func=ACT.Square, bias=eps_t[:, 0:1], scale=1.0)
+                nc.scalar.activation(out=sq_re_eps[i][:], in_=xr[i], func=ACT.Square, bias=eps_t[:, 0:1], scale=1.0)
 
             def square_im_eps(i):
                 sq_im_eps[i] = ahead.tile([P, D], F32, name="hh", tag="hh")
-                nc.scalar.activation(out=sq_im_eps[i][:], in_=xi[i][:], func=ACT.Square, bias=eps_t[:, 0:1], scale=1.0)
+                nc.scalar.activation(out=sq_im_eps[i][:], in_=xi[i], func=ACT.Square, bias=eps_t[:, 0:1], scale=1.0)
 
             def squares(i):
                 sq_re[i] = worka.tile([P, D], F32, name="sr", tag="sr")
-                nc.gpsimd.tensor_tensor(out=sq_re[i][:], in0=xr[i][:], in1=xr[i][:], op=ALU.mult)
                 sq_im[i] = worka.tile([P, D], F32, name="si", tag="si")
-                nc.gpsimd.tensor_tensor(out=sq_im[i][:], in0=xi[i][:], in1=xi[i][:], op=ALU.mult)
+                for dst, src, end in ((sq_re[i], xr[i], D), (sq_im[i], xi[i], GPSIMD_COLS)):
+                    at = 0 if i < SCALAR_SQUARES else end
+                    if at < D:
+                        nc.scalar.activation(out=dst[:, at:D], in_=src[:, at:D], func=ACT.Square)
+                    if at > 0:
+                        nc.gpsimd.tensor_tensor(out=dst[:, 0:at], in0=src[:, 0:at], in1=src[:, 0:at], op=ALU.mult)
+
+            def blocks_of(key):
+                return 4 if key[0] == "r" else min(4, TURNED // P - 4 * key[2])
 
             def flip_sum(key, a, b, h):
                 summed[key] = apsum.tile([P, BANK], F32, name="sum", tag="bank")
-                for jj in range(4):
+                for jj in range(blocks_of(key)):
                     cols = slice(h * BANK + jj * P, h * BANK + (jj + 1) * P)
                     for src, first in ((a, True), (b, False)):
                         nc.tensor.matmul(
@@ -179,12 +191,24 @@ def tile_quantumcoherencelayer_kernel(
             def inverse_n(key):
                 inv[key] = worka.tile([P, BANK], F32, name="in", tag="in")
                 nc.scalar.activation(
-                    out=inv[key][:], in_=summed[key][:], func=ACT.Abs_reciprocal_sqrt, bias=eps_t[:, 0:1], scale=1.0
+                    out=inv[key][:, 0 : P * blocks_of(key)], in_=summed[key][:, 0 : P * blocks_of(key)],
+                    func=ACT.Abs_reciprocal_sqrt, bias=eps_t[:, 0:1], scale=1.0,
+                )
+
+            def add_on_vector(i):
+                rest_n[i] = worka.tile([P, D - TURNED], F32, name="n1", tag="n1")
+                nc.vector.tensor_tensor(
+                    out=rest_n[i][:], in0=sq_re[i][:, TURNED:D], in1=sq_im[i][:, TURNED:D], op=ALU.add
+                )
+
+            def inverse_n_rows(i):
+                nc.scalar.activation(
+                    out=rest_n[i][:], in_=rest_n[i][:], func=ACT.Abs_reciprocal_sqrt, bias=eps_t[:, 0:1], scale=1.0
                 )
 
             def flip_back(key):
                 inv_rows[key] = tpsum.tile([P, BANK], F32, name="bk", tag="bk", bufs=4)
-                for jj in range(4):
+                for jj in range(blocks_of(key)):
                     nc.tensor.transpose(
                         out=inv_rows[key][:, jj * P : (jj + 1) * P], in_=inv[key][:, jj * P : (jj + 1) * P],
                         identity=ident[:],
@@ -192,7 +216,7 @@ def tile_quantumcoherencelayer_kernel(
 
             def transpose_words(i):
                 words[i] = tpsum.tile([P, BANK], F32, name="xt", tag="xt")
-                xw = xr[i][:].bitcast(F32)
+                xw = xr[i].bitcast(F32)
                 for j in range(4):
                     g, u = divmod(j, 2)
                     nc.tensor.transpose(
@@ -201,70 +225,82 @@ def tile_quantumcoherencelayer_kernel(
                     )
 
             def group_words(i):
-                if i % 2 == 0:
-                    grouped[i // 2] = worka.tile(
-                        [P, 2, PASSES, P, 4], BF16, name="grouped", tag="grouped", align_bytes=64
+                if i % 4 == 0:
+                    grouped[i // 4] = worka.tile(
+                        [P, 4, PASSES, P, 4], BF16, name="grouped", tag="grouped", align_bytes=64, bufs=1
                     )
                 nc.scalar.copy(
-                    out=grouped[i // 2][:, i % 2].bitcast(F32),
+                    out=grouped[i // 4][:, i % 4].bitcast(F32),
                     in_=words[i][:].rearrange("p (g u r) -> p g r u", g=PASSES, u=2),
                 )
 
-            def quantize_pair(j):
+            def quantize_four(j):
                 nc.vector.quantize_mx(
-                    out=x_codes[:, 2 * j : 2 * j + 2, :].rearrange("p i c -> p (i c)").bitcast(FP8X4),
-                    scales=x_scales[:, 2 * j : 2 * j + 2, :].rearrange("p i c -> p (i c)"),
+                    out=x_codes[:, 4 * j : 4 * j + 4, :].rearrange("p i c -> p (i c)").bitcast(FP8X4),
+                    scales=x_scales[:, 4 * j : 4 * j + 4, :].rearrange("p i c -> p (i c)"),
                     in_=grouped[j][:].rearrange("p i g r t -> p (i g r t)"),
                 )
 
-            def vector_half(i, h):
+            def coherence_sums(i, h):
                 cols = slice(h * BANK, (h + 1) * BANK)
                 for src, junk, c in ((xr, unit_im_neg, 0), (xi, unit_re, 1)):
                     nc.vector.scalar_tensor_tensor(
                         out=junk[i][:, cols], in0=src[i][:, cols], scalar=EPS, in1=inv_rows[("r", i, h)][:], op0=ALU.add,
                         op1=ALU.mult, accum_out=coh[:, h, c, i : i + 1],
                     )
+
+            def unit_vector(i, at, end, inv_n):
                 nc.vector.scalar_tensor_tensor(
-                    out=unit_im_neg[i][:, cols], in0=xi[i][:, cols], scalar=-1.0, in1=inv_rows[("n", i, h)][:],
+                    out=unit_im_neg[i][:, at:end], in0=xi[i][:, at:end], scalar=-1.0, in1=inv_n[:, 0 : end - at],
                     op0=ALU.mult, op1=ALU.mult,
                 )
                 nc.vector.tensor_tensor(
-                    out=unit_re[i][:, cols], in0=xr[i][:, cols], in1=inv_rows[("n", i, h)][:], op=ALU.mult
+                    out=unit_re[i][:, at:end], in0=xr[i][:, at:end], in1=inv_n[:, 0 : end - at], op=ALU.mult
+                )
+
+            raw_of = [unit_re[NT - 4 + c][:].bitcast(BF16) for c in range(4)]
+            grouped_of = [unit_im_neg[NT - 4 + c][:].bitcast(BF16) for c in range(4)]
+
+            def load_matrix(c):
+                g, h = divmod(c, 2)
+                nc.sync.dma_start(
+                    out=raw_of[c].rearrange("p (t c) -> p t c", t=4),
+                    in_=phase_matrix[512 * g : 512 * (g + 1), BANK * h : BANK * (h + 1)].rearrange(
+                        "(q t) c -> q t c", t=4
+                    ),
+                )
+
+            def quantize_matrix(c):
+                g, h = divmod(c, 2)
+                nc.vector.tensor_copy(
+                    out=grouped_of[c].rearrange("p (c i t) -> p c t i", i=4, t=4),
+                    in_=raw_of[c].rearrange("p (t c i) -> p c t i", t=4, i=4),
+                )
+                nc.vector.quantize_mx(
+                    out=p_codes[:, g, BANK * h : BANK * (h + 1)].bitcast(FP8X4),
+                    scales=p_scales[:, g, BANK * h : BANK * (h + 1)],
+                    in_=grouped_of[c],
                 )
 
             load(0)
             load(1)
             for c in range(4):
-                g, h = divmod(c, 2)
-                raw = unit_re[NT - 4 + c][:].bitcast(BF16)
-                nc.sync.dma_start(
-                    out=raw.rearrange("p (t c) -> p t c", t=4),
-                    in_=phase_matrix[512 * g : 512 * (g + 1), BANK * h : BANK * (h + 1)].rearrange(
-                        "(q t) c -> q t c", t=4
-                    ),
-                )
-                pg = unit_im_neg[NT - 4 + c][:].bitcast(BF16)
-                nc.vector.tensor_copy(
-                    out=pg.rearrange("p (c i t) -> p c t i", i=4, t=4),
-                    in_=raw.rearrange("p (t c i) -> p c t i", t=4, i=4),
-                )
-                nc.vector.quantize_mx(
-                    out=p_codes[:, g, BANK * h : BANK * (h + 1)].bitcast(FP8X4),
-                    scales=p_scales[:, g, BANK * h : BANK * (h + 1)],
-                    in_=pg,
-                )
+                load_matrix(c)
+                quantize_matrix(c)
             load_constants()
 
             for k in range(-2, NT):
                 s, f = k + 2, k + 1
-                if k + 4 < NT:
-                    load(k + 4)
+                if 2 <= k + 3 < NT:
+                    load(k + 3)
                 if s < NT:
                     square_re_eps(s)
                     squares(s)
                 if 0 <= f < NT:
                     flip_sum(("r", f, 0), sq_re_eps[f], sq_im_eps[f], 0)
                     inverse_r(("r", f, 0))
+                    if k >= 0:
+                        inverse_n_rows(k)
                     flip_sum(("n", f, 0), sq_re[f], sq_im[f], 0)
                     inverse_n(("n", f, 0))
                     flip_sum(("r", f, 1), sq_re_eps[f], sq_im_eps[f], 1)
@@ -296,16 +332,22 @@ def tile_quantumcoherencelayer_kernel(
                 if k == 3:
                     nc.vector.tensor_copy(out=wb_cols[:], in_=wbt_ps[:, 0 : 2 * BLOCKS])
                 if k == NT - 1:
+                    inverse_n_rows(k)
                     gains(0, AHEAD)
                     for j in range(AHEAD):
                         product(j)
                         nearest_turns(j)
                         reduced_angle(j)
                 if k >= 0:
-                    vector_half(k, 0)
-                    if k % 2 == 0:
-                        quantize_pair(k // 2)
-                    vector_half(k, 1)
+                    coherence_sums(k, 0)
+                    unit_vector(k, 0, BANK, inv_rows[("n", k, 0)])
+                    coherence_sums(k, 1)
+                    unit_vector(k, BANK, TURNED, inv_rows[("n", k, 1)])
+                    unit_vector(k, TURNED, D, rest_n[k])
+                    if k % 4 == 2:
+                        quantize_four(k // 4)
+                if 0 <= f < NT:
+                    add_on_vector(f)
 
             gains(AHEAD, NT)
 

import math
from contextlib import ExitStack

import concourse.mybir as mybir
from concourse.masks import make_identity

F32 = mybir.dt.float32
BF16 = mybir.dt.bfloat16
I32 = mybir.dt.int32
U32 = mybir.dt.uint32
U8 = mybir.dt.uint8
FP8X4 = mybir.dt.float8_e4m3fn_x4
ACT = mybir.ActivationFunctionType
ALU = mybir.AluOpType

P = 128
D = 1024
ROWS = 2048
NT = ROWS // P
BANK = 512
PASSES = D // 512
BLOCKS = D // P
EPS = 1e-8
POOL_COLS = 704
SCALAR_SQUARES = 3
TURNED = 768
GPSIMD_COLS = 768
AHEAD = 2
FLOPS = 2 * ROWS * D * D


def tile_quantumcoherencelayer_kernel(
    tc, x_real, x_imag, phase_matrix, coherence_factor, ln_weight, ln_bias, out_0, out_1
):
    nc = tc.nc
    xr_d = x_real.flatten_outer_dims().rearrange("(t p) d -> t p d", p=P)
    xi_d = x_imag.flatten_outer_dims().rearrange("(t p) d -> t p d", p=P)
    o0_d = out_0.flatten_outer_dims().rearrange("(t p) d -> t p d", p=P)
    o1_d = out_1.flatten_outer_dims().rearrange("(t p) d -> t p d", p=P)

    with ExitStack() as ctx:
        keep = ctx.enter_context(tc.tile_pool(name="keep", bufs=1))

        ident = keep.tile([P, P], F32)
        make_identity(nc, ident[:])
        eps_t = keep.tile([P, 1], F32)
        nc.vector.memset(eps_t[:], EPS)
        neghalf = keep.tile([P, 2], F32)
        nc.vector.memset(neghalf[:], -0.5)
        warm = keep.tile([P, 1], F32)
        nc.scalar.activation(out=warm[:], in_=eps_t[:], func=ACT.Abs_reciprocal_sqrt)

        cf_bf = keep.tile([P, 1], BF16)
        cf = keep.tile([P, 1], F32)
        cf_turns = keep.tile([P, 1], F32)
        cf_slope = keep.tile([P, 1], F32)

        p_codes = keep.tile([P, PASSES, D], U32, align_bytes=64)
        p_scales = keep.tile([P, PASSES, D], U8, align_bytes=64)
        x_codes = keep.tile([P, NT, PASSES * P], U32, align_bytes=64)
        x_scales = keep.tile([P, NT, PASSES * P], U8, align_bytes=64)
        coh = keep.tile([P, 2, 2, NT], F32)
        gain = keep.tile([P, NT], F32)
        wb_cols = keep.tile([P, 2 * BLOCKS], F32)
        unit_re = [keep.tile([P, D], F32, name="cr%d" % i) for i in range(NT)]
        unit_im_neg = [keep.tile([P, D], F32, name="nci%d" % i, align_bytes=64) for i in range(NT)]

        rows = keep.tile([P, 2 * D], BF16)
        ones = keep.tile([P, P], BF16)

        ahead = ctx.enter_context(tc.tile_pool(name="ahead", bufs=2))
        apsum = ctx.enter_context(tc.psum_pool(name="apsum", bufs=3))
        p0 = {}
        nearest = {}
        sine = {}

        def product(i):
            p0[i] = [apsum.tile([P, BANK], F32, name="p0_%d" % n, tag="bank") for n in range(2)]
            for n in range(2):
                for g in range(PASSES):
                    nc.tensor.matmul_mx(
                        out=p0[i][n][:],
                        lhsT=x_codes[:, i, g * P : (g + 1) * P].bitcast(FP8X4),
                        lhsT_scale=x_scales[:, i, g * P : (g + 1) * P],
                        rhs=p_codes[:, g, n * BANK : (n + 1) * BANK].bitcast(FP8X4),
                        rhs_scale=p_scales[:, g, n * BANK : (n + 1) * BANK],
                        start=(g == 0),
                        stop=(g == PASSES - 1),
                    )

        def nearest_turns(i):
            nearest[i] = ahead.tile([P, D], I32, name="ki", tag="ki", bufs=1)
            for n in range(2):
                cols = slice(n * BANK, (n + 1) * BANK)
                nc.vector.tensor_scalar(
                    out=nearest[i][:, cols], in0=p0[i][n][:], scalar1=gain[:, i : i + 1], scalar2=None, op0=ALU.mult
                )

        def reduced_angle(i):
            sine[i] = ahead.tile([P, D], F32, name="vs", tag="vs")
            for n in range(2):
                cols = slice(n * BANK, (n + 1) * BANK)
                nc.vector.scalar_tensor_tensor(
                    out=sine[i][:, cols], in0=p0[i][n][:], scalar=gain[:, i : i + 1], in1=nearest[i][:, cols],
                    op0=ALU.mult, op1=ALU.subtract,
                )

        def gains(first, end):
            both = coh[:, 0, :, first:end]
            nc.vector.tensor_tensor(out=both, in0=both, in1=coh[:, 1, :, first:end], op=ALU.add)
            nc.vector.tensor_tensor(out=both, in0=both, in1=both, op=ALU.mult)
            nc.vector.tensor_tensor(
                out=coh[:, 0, 0, first:end], in0=coh[:, 0, 0, first:end], in1=coh[:, 0, 1, first:end], op=ALU.add
            )
            nc.vector.tensor_scalar(
                out=gain[:, first:end], in0=coh[:, 0, 0, first:end], scalar1=cf_slope[:, 0:1], scalar2=cf_turns[:, 0:1],
                op0=ALU.mult, op1=ALU.add,
            )

        with tc.tile_pool(name="stage", bufs=1) as stage, tc.tile_pool(name="xin", bufs=4) as xin, tc.tile_pool(
            name="worka", bufs=2
        ) as worka, tc.psum_pool(name="tpsum", bufs=1) as tpsum, tc.manual_schedule():
            nc.gpsimd.memset(rows[:], 0.0)
            nc.gpsimd.memset(ones[:], 1.0)
            wb = stage.tile([P, P], BF16)
            nc.gpsimd.memset(wb[:], 0.0)
            wb32 = stage.tile([P, P], F32)
            xr = {}
            xi = {}
            sq_re_eps = {}
            sq_im_eps = {}
            sq_re = {}
            sq_im = {}
            summed = {}
            inv = {}
            rest_n = {}
            inv_rows = {}
            words = {}
            grouped = {}

            def load_constants():
                with nc.allow_non_contiguous_dma(reason="one bfloat16 scalar to every partition"):
                    nc.sync.dma_start(out=cf_bf[:], in_=coherence_factor.partition_broadcast(P))
                nc.sync.dma_start(out=rows[0:1, 0:D], in_=ln_weight.rearrange("(o d) -> o d", o=1))
                nc.sync.dma_start(out=rows[0:1, D : 2 * D], in_=ln_bias.rearrange("(o d) -> o d", o=1))
                nc.sync.dma_start(out=wb[0:BLOCKS, :], in_=ln_weight.rearrange("(j p) -> j p", p=P))
                nc.sync.dma_start(out=wb[BLOCKS : 2 * BLOCKS, :], in_=ln_bias.rearrange("(j p) -> j p", p=P))

            def load(i):
                both = xin.tile([P, 2, D], BF16, name="x", tag="x")
                xr[i] = both[:, 0, :]
                xi[i] = both[:, 1, :]
                nc.sync.dma_start(out=xr[i], in_=xr_d[i])
                nc.sync.dma_start(out=xi[i], in_=xi_d[i])

            def square_re_eps(i):
                sq_re_eps[i] = ahead.tile([P, D], F32, name="vs", tag="vs")
                nc.scalar.activation(out=sq_re_eps[i][:], in_=xr[i], func=ACT.Square, bias=eps_t[:, 0:1], scale=1.0)

            def square_im_eps(i):
                sq_im_eps[i] = ahead.tile([P, D], F32, name="hh", tag="hh")
                nc.scalar.activation(out=sq_im_eps[i][:], in_=xi[i], func=ACT.Square, bias=eps_t[:, 0:1], scale=1.0)

            def squares(i):
                sq_re[i] = worka.tile([P, D], F32, name="sr", tag="sr")
                sq_im[i] = worka.tile([P, D], F32, name="si", tag="si")
                for dst, src, end in ((sq_re[i], xr[i], D), (sq_im[i], xi[i], GPSIMD_COLS)):
                    at = 0 if i < SCALAR_SQUARES else end
                    if at < D:
                        nc.scalar.activation(out=dst[:, at:D], in_=src[:, at:D], func=ACT.Square)
                    if at > 0:
                        nc.gpsimd.tensor_tensor(out=dst[:, 0:at], in0=src[:, 0:at], in1=src[:, 0:at], op=ALU.mult)

            def blocks_of(key):
                return 4 if key[0] == "r" else min(4, TURNED // P - 4 * key[2])

            def flip_sum(key, a, b, h):
                summed[key] = apsum.tile([P, BANK], F32, name="sum", tag="bank")
                for jj in range(blocks_of(key)):
                    cols = slice(h * BANK + jj * P, h * BANK + (jj + 1) * P)
                    for src, first in ((a, True), (b, False)):
                        nc.tensor.matmul(
                            out=summed[key][:, jj * P : (jj + 1) * P], lhsT=src[:, cols], rhs=ident[:], start=first,
                            stop=not first, is_transpose=True,
                        )

            def inverse_r(key):
                inv[key] = worka.tile([P, BANK], F32, name="ir", tag="ir")
                nc.scalar.activation(out=inv[key][:], in_=summed[key][:], func=ACT.Abs_reciprocal_sqrt)

            def inverse_n(key):
                inv[key] = worka.tile([P, BANK], F32, name="in", tag="in")
                nc.scalar.activation(
                    out=inv[key][:, 0 : P * blocks_of(key)], in_=summed[key][:, 0 : P * blocks_of(key)],
                    func=ACT.Abs_reciprocal_sqrt, bias=eps_t[:, 0:1], scale=1.0,
                )

            def add_on_vector(i):
                rest_n[i] = worka.tile([P, D - TURNED], F32, name="n1", tag="n1")
                nc.vector.tensor_tensor(
                    out=rest_n[i][:], in0=sq_re[i][:, TURNED:D], in1=sq_im[i][:, TURNED:D], op=ALU.add
                )

            def inverse_n_rows(i):
                nc.scalar.activation(
                    out=rest_n[i][:], in_=rest_n[i][:], func=ACT.Abs_reciprocal_sqrt, bias=eps_t[:, 0:1], scale=1.0
                )

            def flip_back(key):
                inv_rows[key] = tpsum.tile([P, BANK], F32, name="bk", tag="bk", bufs=4)
                for jj in range(blocks_of(key)):
                    nc.tensor.transpose(
                        out=inv_rows[key][:, jj * P : (jj + 1) * P], in_=inv[key][:, jj * P : (jj + 1) * P],
                        identity=ident[:],
                    )

            def transpose_words(i):
                words[i] = tpsum.tile([P, BANK], F32, name="xt", tag="xt")
                xw = xr[i].bitcast(F32)
                for j in range(4):
                    g, u = divmod(j, 2)
                    nc.tensor.transpose(
                        out=words[i][:, j * P : (j + 1) * P], in_=xw[:, 256 * g + u : 256 * (g + 1) : 2],
                        identity=ident[:],
                    )

            def group_words(i):
                if i % 4 == 0:
                    grouped[i // 4] = worka.tile(
                        [P, 4, PASSES, P, 4], BF16, name="grouped", tag="grouped", align_bytes=64, bufs=1
                    )
                nc.scalar.copy(
                    out=grouped[i // 4][:, i % 4].bitcast(F32),
                    in_=words[i][:].rearrange("p (g u r) -> p g r u", g=PASSES, u=2),
                )

            def quantize_four(j):
                nc.vector.quantize_mx(
                    out=x_codes[:, 4 * j : 4 * j + 4, :].rearrange("p i c -> p (i c)").bitcast(FP8X4),
                    scales=x_scales[:, 4 * j : 4 * j + 4, :].rearrange("p i c -> p (i c)"),
                    in_=grouped[j][:].rearrange("p i g r t -> p (i g r t)"),
                )

            def coherence_sums(i, h):
                cols = slice(h * BANK, (h + 1) * BANK)
                for src, junk, c in ((xr, unit_im_neg, 0), (xi, unit_re, 1)):
                    nc.vector.scalar_tensor_tensor(
                        out=junk[i][:, cols], in0=src[i][:, cols], scalar=EPS, in1=inv_rows[("r", i, h)][:], op0=ALU.add,
                        op1=ALU.mult, accum_out=coh[:, h, c, i : i + 1],
                    )

            def unit_vector(i, at, end, inv_n):
                nc.vector.scalar_tensor_tensor(
                    out=unit_im_neg[i][:, at:end], in0=xi[i][:, at:end], scalar=-1.0, in1=inv_n[:, 0 : end - at],
                    op0=ALU.mult, op1=ALU.mult,
                )
                nc.vector.tensor_tensor(
                    out=unit_re[i][:, at:end], in0=xr[i][:, at:end], in1=inv_n[:, 0 : end - at], op=ALU.mult
                )

            raw_of = [unit_re[NT - 4 + c][:].bitcast(BF16) for c in range(4)]
            grouped_of = [unit_im_neg[NT - 4 + c][:].bitcast(BF16) for c in range(4)]

            def load_matrix(c):
                g, h = divmod(c, 2)
                nc.sync.dma_start(
                    out=raw_of[c].rearrange("p (t c) -> p t c", t=4),
                    in_=phase_matrix[512 * g : 512 * (g + 1), BANK * h : BANK * (h + 1)].rearrange(
                        "(q t) c -> q t c", t=4
                    ),
                )

            def quantize_matrix(c):
                g, h = divmod(c, 2)
                nc.vector.tensor_copy(
                    out=grouped_of[c].rearrange("p (c i t) -> p c t i", i=4, t=4),
                    in_=raw_of[c].rearrange("p (t c i) -> p c t i", t=4, i=4),
                )
                nc.vector.quantize_mx(
                    out=p_codes[:, g, BANK * h : BANK * (h + 1)].bitcast(FP8X4),
                    scales=p_scales[:, g, BANK * h : BANK * (h + 1)],
                    in_=grouped_of[c],
                )

            load(0)
            load(1)
            for c in range(4):
                load_matrix(c)
                quantize_matrix(c)
            load_constants()

            for k in range(-2, NT):
                s, f = k + 2, k + 1
                if 2 <= k + 3 < NT:
                    load(k + 3)
                if s < NT:
                    square_re_eps(s)
                    squares(s)
                if 0 <= f < NT:
                    flip_sum(("r", f, 0), sq_re_eps[f], sq_im_eps[f], 0)
                    inverse_r(("r", f, 0))
                    if k >= 0:
                        inverse_n_rows(k)
                    flip_sum(("n", f, 0), sq_re[f], sq_im[f], 0)
                    inverse_n(("n", f, 0))
                    flip_sum(("r", f, 1), sq_re_eps[f], sq_im_eps[f], 1)
                if s < NT:
                    square_im_eps(s)
                    transpose_words(s)
                if 0 <= f < NT:
                    inverse_r(("r", f, 1))
                    flip_back(("r", f, 0))
                    flip_back(("n", f, 0))
                    flip_sum(("n", f, 1), sq_re[f], sq_im[f], 1)
                    inverse_n(("n", f, 1))
                if s < NT:
                    group_words(s)
                if 0 <= f < NT:
                    flip_back(("r", f, 1))
                    flip_back(("n", f, 1))
                if k == 2:
                    nc.vector.tensor_copy(out=cf[:], in_=cf_bf[:])
                    nc.vector.tensor_scalar(
                        out=cf_turns[:], in0=cf[:], scalar1=1.0 / (2.0 * math.pi), scalar2=None, op0=ALU.mult
                    )
                    nc.vector.tensor_scalar(
                        out=cf_slope[:], in0=cf[:], scalar1=-1.0 / (2.0 * math.pi * D * D), scalar2=None, op0=ALU.mult
                    )
                    nc.vector.tensor_copy(out=wb32[:], in_=wb[:])
                    wbt_ps = apsum.tile([P, BANK], F32, name="wbt", tag="bank")
                    nc.tensor.transpose(out=wbt_ps[:, 0:P], in_=wb32[:], identity=ident[:])
                if k == 3:
                    nc.vector.tensor_copy(out=wb_cols[:], in_=wbt_ps[:, 0 : 2 * BLOCKS])
                if k == NT - 1:
                    inverse_n_rows(k)
                    gains(0, AHEAD)
                    for j in range(AHEAD):
                        product(j)
                        nearest_turns(j)
                        reduced_angle(j)
                if k >= 0:
                    coherence_sums(k, 0)
                    unit_vector(k, 0, BANK, inv_rows[("n", k, 0)])
                    coherence_sums(k, 1)
                    unit_vector(k, BANK, TURNED, inv_rows[("n", k, 1)])
                    unit_vector(k, TURNED, D, rest_n[k])
                    if k % 4 == 2:
                        quantize_four(k // 4)
                if 0 <= f < NT:
                    add_on_vector(f)

            gains(AHEAD, NT)

        with tc.tile_pool(name="workb", bufs=2) as workb, tc.tile_pool(name="stat", bufs=4) as stat, tc.psum_pool(
            name="ppsum", bufs=2
        ) as ppsum, tc.manual_schedule():
            w_ps = ppsum.tile([P, D], BF16, name="w_ps", tag="w_ps", bufs=1)
            b_ps = ppsum.tile([P, D], BF16, name="b_ps", tag="b_ps", bufs=1)
            for dst, at in ((w_ps, 0), (b_ps, D)):
                for h in range(2):
                    nc.tensor.matmul(
                        out=dst[:, h * BANK : (h + 1) * BANK], lhsT=ones[:],
                        rhs=rows[:, at + h * BANK : at + (h + 1) * BANK], start=True, stop=True,
                    )
            vers = {}
            out_re = {}
            cos_im = {}
            rot_im = {}
            rot_re = {}
            sums = {}
            neg_mean = {}
            sq_dev = {}
            var_eps = {}
            inv_std = {}
            turned_im = {}

            def valid(i):
                return 0 <= i < NT

            def turned(i):
                return 0 <= i < NT - 1

            def two_sines(i):
                vers[i] = ahead.tile([P, D], F32, name="hh", tag="hh")
                nc.scalar.activation(out=vers[i][:], in_=sine[i][:], func=ACT.Sin, scale=math.pi)
                nc.scalar.activation(out=sine[i][:], in_=sine[i][:], func=ACT.Sin, scale=2.0 * math.pi)

            def versine(i):
                nc.scalar.activation(out=vers[i][:], in_=vers[i][:], func=ACT.Square, scale=math.sqrt(2.0))

            def cosine_products_and_real_part(i):
                out_re[i] = workb.tile([P, D], F32, name="fa", tag="fa", bufs=3)
                cos_im[i] = workb.tile([P, D], F32, name="fb", tag="o%d" % (i % 4), bufs=1)
                nc.vector.scalar_tensor_tensor(
                    out=out_re[i][:], in0=vers[i][:], scalar=1.0, in1=unit_re[i][:], op0=ALU.subtract, op1=ALU.mult
                )
                nc.vector.scalar_tensor_tensor(
                    out=cos_im[i][:], in0=vers[i][:], scalar=1.0, in1=unit_im_neg[i][:], op0=ALU.subtract, op1=ALU.mult
                )
                sums[i] = stat.tile([P, 2], F32, name="sums", tag="sums")
                nc.vector.scalar_tensor_tensor(
                    out=rot_re[i][:], in0=rot_re[i][:], scalar=1.0, in1=out_re[i][:], op0=ALU.mult, op1=ALU.subtract,
                    accum_out=sums[i][:, 0:1],
                )

            def sine_product_re_on_vector(i):
                rot_re[i] = workb.tile([P, D], F32, name="sb2", tag="sb2", bufs=3)
                nc.vector.tensor_tensor(
                    out=rot_re[i][:, POOL_COLS:D], in0=sine[i][:, POOL_COLS:D], in1=unit_im_neg[i][:, POOL_COLS:D],
                    op=ALU.mult,
                )

            def normalise_im(i):
                nc.vector.tensor_scalar(
                    out=rot_im[i][:], in0=rot_im[i][:], scalar1=neg_mean[i][:, 1:2], scalar2=inv_std[i][:, 1:2],
                    op0=ALU.add, op1=ALU.mult,
                )

            def imaginary_part(i):
                nc.vector.scalar_tensor_tensor(
                    out=rot_im[i][:], in0=rot_im[i][:], scalar=1.0, in1=cos_im[i][:], op0=ALU.mult, op1=ALU.add,
                    accum_out=sums[i][:, 1:2],
                )

            def variances(i):
                neg_mean[i] = stat.tile([P, 2], F32, name="nmu", tag="nmu")
                nc.scalar.activation(out=neg_mean[i][:], in_=sums[i][:], func=ACT.Identity, scale=-1.0 / D)
                sq_dev[i] = stat.tile([P, 2], F32, name="sq", tag="sq")
                nc.scalar.activation(
                    out=vers[i][:], in_=rot_re[i][:], func=ACT.Square, bias=neg_mean[i][:, 0:1], scale=1.0,
                    accum_out=sq_dev[i][:, 0:1],
                )
                nc.scalar.activation(
                    out=vers[i][:], in_=rot_im[i][:], func=ACT.Square, bias=neg_mean[i][:, 1:2], scale=1.0,
                    accum_out=sq_dev[i][:, 1:2],
                )
                var_eps[i] = stat.tile([P, 2], F32, name="var", tag="var")
                nc.scalar.activation(
                    out=var_eps[i][:], in_=sq_dev[i][:], func=ACT.Identity, bias=eps_t[:, 0:1], scale=1.0 / D
                )

            def sine_products_on_gpsimd(i):
                rot_im[i] = workb.tile([P, D], F32, name="sa2", tag="o%d" % ((i - 1) % 4), bufs=1)
                nc.gpsimd.tensor_tensor(out=rot_im[i][:], in0=sine[i][:], in1=unit_re[i][:], op=ALU.mult)
                nc.gpsimd.tensor_tensor(
                    out=rot_re[i][:, 0:POOL_COLS], in0=sine[i][:, 0:POOL_COLS], in1=unit_im_neg[i][:, 0:POOL_COLS],
                    op=ALU.mult,
                )

            def inverse_deviations(i):
                inv_std[i] = stat.tile([P, 2], F32, name="rstd", tag="rstd")
                nc.gpsimd.tensor_tensor(out=inv_std[i][:], in0=var_eps[i][:], in1=neghalf[:], op=ALU.pow)

            def scale(dst, src, i, c):
                nc.vector.scalar_tensor_tensor(
                    out=dst[:], in0=src[:], scalar=neg_mean[i][:, c : c + 1], in1=w_ps[:], op0=ALU.add, op1=ALU.mult
                )

            def shift(dst, i, c):
                nc.vector.scalar_tensor_tensor(
                    out=dst[:], in0=dst[:], scalar=inv_std[i][:, c : c + 1], in1=b_ps[:], op0=ALU.mult, op1=ALU.add
                )

            def there(i, half):
                t1 = ppsum.tile([P, BANK], F32, name="t1", tag="t1", bufs=1)
                for jj in range(4):
                    j = 4 * half + jj
                    nc.tensor.transpose(
                        out=t1[:, jj * P : (jj + 1) * P], in_=rot_im[i][:, j * P : (j + 1) * P], identity=ident[:]
                    )
                for jj in range(4):
                    j = 4 * half + jj
                    nc.scalar.activation(
                        out=turned_im[i][:, j, :], in_=t1[:, jj * P : (jj + 1) * P], func=ACT.Identity,
                        bias=wb_cols[:, BLOCKS + j : BLOCKS + j + 1], scale=wb_cols[:, j : j + 1],
                    )

            def back(i, half):
                t2 = ppsum.tile([P, BANK], F32, name="t2", tag="t2", bufs=1)
                for jj in range(4):
                    j = 4 * half + jj
                    nc.tensor.transpose(out=t2[:, jj * P : (jj + 1) * P], in_=turned_im[i][:, j, :], identity=ident[:])
                nc.scalar.copy(out=rot_im[i][:, half * BANK : (half + 1) * BANK], in_=t2[:])

            for k in range(-1, NT + 1):
                if valid(k + 1):
                    two_sines(k + 1)
                if turned(k - 2):
                    back(k - 2, 1)
                    nc.sync.dma_start(out=o1_d[k - 2], in_=rot_im[k - 2][:])
                if AHEAD <= k + 2 < NT:
                    product(k + 2)
                if valid(k):
                    cosine_products_and_real_part(k)
                if valid(k + 1):
                    sine_product_re_on_vector(k + 1)
                if turned(k - 1):
                    normalise_im(k - 1)
                if valid(k):
                    imaginary_part(k)
                if valid(k + 1):
                    versine(k + 1)
                if turned(k - 1):
                    turned_im[k - 1] = workb.tile([P, BLOCKS, P], F32, name="ot", tag="ot", bufs=1)
                    there(k - 1, 0)
                if valid(k):
                    variances(k)
                if turned(k - 1):
                    back(k - 1, 0)
                    there(k - 1, 1)
                if valid(k - 1):
                    scale(out_re[k - 1], rot_re[k - 1], k - 1, 0)
                if k - 1 == NT - 1:
                    scale(rot_im[k - 1], rot_im[k - 1], k - 1, 1)
                if AHEAD <= k + 2 < NT:
                    nearest_turns(k + 2)
                if valid(k - 1):
                    shift(out_re[k - 1], k - 1, 0)
                    nc.sync.dma_start(out=o0_d[k - 1], in_=out_re[k - 1][:])
                if k - 1 == NT - 1:
                    shift(rot_im[k - 1], k - 1, 1)
                    nc.sync.dma_start(out=o1_d[k - 1], in_=rot_im[k - 1][:])
                if valid(k + 1):
                    sine_products_on_gpsimd(k + 1)
                if valid(k):
                    inverse_deviations(k)
                if AHEAD <= k + 2 < NT:
                    reduced_angle(k + 2)
